import numpy as np
import ml_dtypes


def mxq(x, axis, fmt="e4m3"):
    dtype, down = {"e4m3": (ml_dtypes.float8_e4m3fn, 7), "e5m2": (ml_dtypes.float8_e5m2, 14)}[fmt]
    v = np.moveaxis(np.asarray(x, np.float32).astype(ml_dtypes.bfloat16).astype(np.float64), axis, -1)
    blocks = v.reshape(v.shape[:-1] + (-1, 32))
    amax = np.abs(blocks).max(-1, keepdims=True)
    byte = np.maximum(np.where(amax > 0, np.frexp(amax)[1] - 1 + 127, 0) - down, 1)
    scale = np.exp2(byte - 127.0)
    codes = (blocks / scale).astype(np.float32).astype(dtype).astype(np.float64)
    return np.moveaxis((codes * scale).reshape(v.shape), -1, axis)


WIDE = False


def mx_kscale(k):
    if not WIDE:
        return np.ones(k)
    levels = np.array([10, -10, 5, -5, 0])
    a = np.random.permutation(np.resize(levels, k // 512 * 4)).reshape(k // 512, 4)
    idx = np.arange(k)
    return np.exp2(a[idx // 512, idx % 128 // 32])


BF16 = ml_dtypes.bfloat16


def bf(x):
    return np.asarray(x, np.float32).astype(BF16)


def f64(x):
    return np.asarray(x).astype(np.float64)


B, H, N, NMAX, NMIN, V, VI, NH = 4096, 512, 127, 127, 126, 16, 3, 2
TS = 4.0


def distortion(X):
    cols = [np.sum(X[:, :-k] * X[:, k:], axis=1) for k in range(1, N + 1)]
    return np.stack(cols[::-1], axis=1)


def setup_inputs():
    s, t = mx_kscale(H), mx_kscale(H)
    return {"h1": bf(np.maximum(np.random.standard_normal((B, H)), 0.0) * s),
            "w_hid2": bf(np.random.standard_normal((H, H)) * 1.5 / np.sqrt(H) * t[:, None] / s[None, :]),
            "b_hid2": bf(np.random.standard_normal(H) * 0.2 * t),
            "w_out": bf(np.random.standard_normal((N + 1, H)) * 0.18 / np.sqrt(H) / t[None, :]),
            "b_out": bf(np.random.standard_normal(N + 1) * 0.03),
            "norm_root": bf(np.sqrt(TS * np.sqrt(N)) * np.exp(0.15 * np.random.standard_normal((B, 1)))),
            "T": bf(np.random.standard_normal((B, N)) * TS)}


def reference(h1, w_hid2, b_hid2, w_out, b_out, norm_root, T):
    h2 = np.maximum((mxq(f64(h1), 1, "e4m3") @ mxq(f64(w_hid2), 1, "e4m3").T) + f64(b_hid2), 0.0)
    X_hat = ((mxq(h2, 1, "e4m3") @ mxq(f64(w_out), 1, "e4m3").T) + f64(b_out)) * f64(norm_root)
    X_hat_clamped = np.clip(X_hat, -2.0, 2.0)
    error = np.reshape(np.mean((distortion(X_hat) - f64(T)) ** 2), (1,))
    error_clamped = np.reshape(np.mean((distortion(X_hat_clamped) - f64(T)) ** 2), (1,))
    return (X_hat, error, X_hat_clamped, error_clamped)

@@ -1,0 +1,154 @@
+from contextlib import ExitStack
+
+import concourse.mybir as mybir
+from concourse.masks import make_identity
+
+F32 = mybir.dt.float32
+BF16 = mybir.dt.bfloat16
+U32 = mybir.dt.uint32
+U8 = mybir.dt.uint8
+FP8X4 = mybir.dt.float8_e4m3fn_x4
+ALU = mybir.AluOpType
+AF = mybir.ActivationFunctionType
+AX = mybir.AxisListType
+
+P = 128
+B = 4096
+H = 512
+N = 128
+LAGS = 127
+TILES = B // P
+BLK = 4
+NBLK = TILES // BLK
+
+FLOPS = 2 * B * H * (H + N) + 2 * 2 * B * (N * LAGS // 2)
+
+
+def tile_qdtssolveronnx_pa_kernel(tc, h1, w_hid2, b_hid2, w_out, b_out, norm_root, T, out_0, out_1, out_2, out_3):
+    nc = tc.nc
+    with ExitStack() as ctx:
+        keep = ctx.enter_context(tc.tile_pool(name="keep", bufs=1))
+        stage = ctx.enter_context(tc.tile_pool(name="stage", bufs=2))
+        work = ctx.enter_context(tc.tile_pool(name="work", bufs=2))
+        ps_tp = ctx.enter_context(tc.psum_pool(name="ps_tp", bufs=2))
+        ps_m1 = ctx.enter_context(tc.psum_pool(name="ps_m1", bufs=4))
+        ps_m2 = ctx.enter_context(tc.psum_pool(name="ps_m2", bufs=1))
+        ps_y = ctx.enter_context(tc.psum_pool(name="ps_y", bufs=1))
+
+        w1_sb = keep.tile([P, 4, H], BF16)
+        nc.sync.dma_start(out=w1_sb[:], in_=w_hid2.rearrange("(p c) k -> p c k", c=4))
+        h1_sb = keep.tile([P, TILES, H], BF16)
+        h1_v = h1.rearrange("(p t) k -> p t k", t=TILES)
+        nc.sync.dma_start(out=h1_sb[:, 0:BLK, :], in_=h1_v[:, 0:BLK, :])
+        w2_sb = keep.tile([P, H], BF16)
+        nc.sync.dma_start(out=w2_sb[:], in_=w_out)
+        b1_bf = keep.tile([P, 4], BF16)
+        b2_bf = keep.tile([P, 1], BF16)
+        nr_bf = keep.tile([P, TILES], BF16)
+        with nc.allow_non_contiguous_dma(reason="three short vectors, a few bytes a partition"):
+            nc.scalar.dma_start(out=b1_bf[:], in_=b_hid2.rearrange("(p c) -> p c", c=4))
+            nc.scalar.dma_start(out=b2_bf[:], in_=b_out.rearrange("(p o) -> p o", o=1))
+            nc.scalar.dma_start(out=nr_bf[:], in_=norm_root.rearrange("(p t) o -> p (t o)", t=TILES))
+        for i in range(1, NBLK):
+            nc.sync.dma_start(out=h1_sb[:, BLK * i:BLK * (i + 1), :], in_=h1_v[:, BLK * i:BLK * (i + 1), :])
+        t_sb = keep.tile([P, TILES, LAGS], BF16)
+        nc.sync.dma_start(out=t_sb[:], in_=T.rearrange("(p t) c -> p t c", t=TILES))
+
+        ident = keep.tile([P, P], F32)
+        make_identity(nc, ident[:])
+        b1 = keep.tile([P, 4], F32)
+        nc.vector.tensor_copy(out=b1[:], in_=b1_bf[:])
+        b2 = keep.tile([P, 1], F32)
+        nc.vector.tensor_copy(out=b2[:], in_=b2_bf[:])
+        nr = keep.tile([P, TILES], F32)
+        nc.vector.tensor_copy(out=nr[:], in_=nr_bf[:])
+
+        w1g = keep.tile([P, 4 * P, 4], BF16, align_bytes=64)
+        w1g32 = w1g[:].bitcast(F32)
+        w1_32 = w1_sb[:].bitcast(F32)
+        for a in range(2):
+            pw = ps_tp.tile([P, 2, 2, P], F32, tag="tp")
+            for u in range(2):
+                for cc in range(2):
+                    nc.tensor.transpose(pw[:, u, cc, :], w1_32[:, 2 * a + cc, P * u:P * (u + 1)], ident[:])
+            nc.vector.tensor_copy(out=w1g32[:, 2 * P * a:2 * P * (a + 1), :], in_=pw[:].rearrange("q u c m -> q (c m) u"))
+        w1c = keep.tile([P, 4 * P], U32, align_bytes=64)
+        w1s = keep.tile([P, 4 * P], U8, align_bytes=64)
+        nc.vector.quantize_mx(out=w1c[:].bitcast(FP8X4), scales=w1s[:], in_=w1g[:].rearrange("q n f -> q (n f)"))
+
+        w2g = keep.tile([P, P, 4], BF16, align_bytes=64)
+        w2_32 = w2_sb[:].bitcast(F32).rearrange("p (m u) -> p u m", u=2)
+        pw2 = ps_tp.tile([P, 2, P], F32, tag="tp")
+        for u in range(2):
+            nc.tensor.transpose(pw2[:, u, :], w2_32[:, u, :], ident[:])
+        nc.vector.tensor_copy(out=w2g[:].bitcast(F32), in_=pw2[:].rearrange("q u n -> q n u"))
+        w2c = keep.tile([P, P], U32, align_bytes=64)
+        w2s = keep.tile([P, P], U8, align_bytes=64)
+        nc.vector.quantize_mx(out=w2c[:].bitcast(FP8X4), scales=w2s[:], in_=w2g[:].rearrange("q n f -> q (n f)"))
+
+        xr = keep.tile([P, TILES, N], F32)
+        xc = keep.tile([P, TILES, N], F32)
+        o0 = out_0.rearrange("(p t) j -> p t j", t=TILES)
+        o2 = out_2.rearrange("(p t) j -> p t j", t=TILES)
+        h1_32 = h1_sb[:].bitcast(F32)
+
+        for i in range(NBLK):
+            h1g = stage.tile([P, BLK * P, 4], BF16, align_bytes=64)
+            h1g32 = h1g[:].bitcast(F32)
+            for a in range(2):
+                pt = ps_tp.tile([P, 2, 2, P], F32, tag="tp")
+                for u in range(2):
+                    for tt in range(2):
+                        nc.tensor.transpose(pt[:, u, tt, :], h1_32[:, BLK * i + 2 * a + tt, P * u:P * (u + 1)], ident[:])
+                nc.scalar.copy(out=h1g32[:, 2 * P * a:2 * P * (a + 1), :], in_=pt[:].rearrange("q u t p -> q (t p) u"))
+            h1c = stage.tile([P, BLK * P], U32, align_bytes=64)
+            h1s = stage.tile([P, BLK * P], U8, align_bytes=64)
+            nc.vector.quantize_mx(out=h1c[:].bitcast(FP8X4), scales=h1s[:], in_=h1g[:].rearrange("q n f -> q (n f)"))
+
+            h2p = stage.tile([P, 4, BLK * P], BF16)
+            for c in range(4):
+                p1 = ps_m1.tile([P, BLK * P], F32, tag="m1")
+                nc.tensor.matmul_mx(out=p1[:], lhsT=w1c[:, P * c:P * (c + 1)].bitcast(FP8X4), lhsT_scale=w1s[:, P * c:P * (c + 1)],
+                                    rhs=h1c[:].bitcast(FP8X4), rhs_scale=h1s[:], start=True, stop=True)
+                nc.scalar.activation(out=h2p[:, c, :], in_=p1[:], func=AF.Relu, bias=b1[:, c:c + 1], scale=1.0)
+            h2g = stage.tile([P, BLK * P, 4], BF16, align_bytes=64)
+            nc.vector.tensor_copy(out=h2g[:], in_=h2p[:].rearrange("m c n -> m n c"))
+            h2c = stage.tile([P, BLK * P], U32, align_bytes=64)
+            h2s = stage.tile([P, BLK * P], U8, align_bytes=64)
+            nc.vector.quantize_mx(out=h2c[:].bitcast(FP8X4), scales=h2s[:], in_=h2g[:].rearrange("m n f -> m (n f)"))
+
+            p2 = ps_m2.tile([P, BLK * P], F32, tag="m2")
+            nc.tensor.matmul_mx(out=p2[:], lhsT=w2c[:].bitcast(FP8X4), lhsT_scale=w2s[:],
+                                rhs=h2c[:].bitcast(FP8X4), rhs_scale=h2s[:], start=True, stop=True)
+            yt = stage.tile([P, BLK * P], F32)
+            nc.scalar.activation(out=yt[:], in_=p2[:], func=AF.Identity, bias=b2[:, 0:1], scale=1.0)
+            py = ps_y.tile([P, BLK, P], F32, tag="py")
+            for t in range(BLK):
+                nc.tensor.transpose(py[:, t, :], yt[:, P * t:P * (t + 1)], ident[:])
+            for t in range(BLK):
+                g = BLK * i + t
+                nc.scalar.activation(out=xr[:, g, :], in_=py[:, t, :], func=AF.Copy, scale=nr[:, g:g + 1])
+            blk = slice(BLK * i, BLK * (i + 1))
+            nc.gpsimd.tensor_scalar(out=xc[:, blk, :], in0=xr[:, blk, :], scalar1=-2.0, scalar2=2.0, op0=ALU.max, op1=ALU.min)
+            nc.sync.dma_start(out=o0[:, blk, :], in_=xr[:, blk, :])
+            nc.sync.dma_start(out=o2[:, blk, :], in_=xc[:, blk, :])
+
+        sums = keep.tile([P, P], F32)
+        nc.vector.memset(sums[:], 0.0)
+        for s, sig in enumerate((xr, xc)):
+            z = work.tile([P, TILES, LAGS], F32, tag="z")
+            for k in range(1, N):
+                prod = work.tile([P, TILES, LAGS], F32, tag="prod")
+                nc.vector.tensor_tensor(out=prod[:, :, 0:N - k], in0=sig[:, :, 0:N - k], in1=sig[:, :, k:N], op=ALU.mult)
+                nc.vector.tensor_reduce(out=z[:, :, LAGS - k:LAGS - k + 1], in_=prod[:, :, 0:N - k], axis=AX.X, op=ALU.add)
+            nc.vector.tensor_tensor(out=z[:], in0=z[:], in1=t_sb[:], op=ALU.subtract)
+            sq = work.tile([P, TILES, LAGS], F32, tag="prod")
+            nc.scalar.activation(out=sq[:], in_=z[:], func=AF.Square, accum_out=sums[:, s:s + 1])
+        pf = ps_y.tile([P, P], F32, tag="py")
+        nc.tensor.transpose(pf[:], sums[:], ident[:])
+        tot = keep.tile([P, 1], F32)
+        nc.vector.tensor_reduce(out=tot[:], in_=pf[:], axis=AX.X, op=ALU.add)
+        res = keep.tile([P, 1], F32)
+        nc.vector.tensor_scalar(out=res[:], in0=tot[:], scalar1=1.0 / (B * LAGS), scalar2=None, op0=ALU.mult)
+        nc.sync.dma_start(out=out_1.rearrange("(a b) -> a b", a=1), in_=res[0:1, 0:1])
+        nc.sync.dma_start(out=out_3.rearrange("(a b) -> a b", a=1), in_=res[1:2, 0:1])

@@ -1,3 +1,4 @@
+import math
 from contextlib import ExitStack
 
 import concourse.mybir as mybir
@@ -5,6 +6,7 @@ from concourse.masks import make_identity
 
 F32 = mybir.dt.float32
 BF16 = mybir.dt.bfloat16
+I32 = mybir.dt.int32
 U32 = mybir.dt.uint32
 U8 = mybir.dt.uint8
 FP8X4 = mybir.dt.float8_e4m3fn_x4
@@ -20,6 +22,10 @@ LAGS = 127
 TILES = B // P
 BLK = 4
 NBLK = TILES // BLK
+BATCHES = ((0, 1), (1, 2), (3, 2), (5, 2), (7, 1))
+NB = len(BATCHES)
+TBMAX = 8
+G = 64
 
 FLOPS = 2 * B * H * (H + N) + 2 * 2 * B * (N * LAGS // 2)
 
@@ -28,20 +34,19 @@ def tile_qdtssolveronnx_pa_kernel(tc, h1, w_hid2, b_hid2, w_out, b_out, norm_roo
     nc = tc.nc
     with ExitStack() as ctx:
         keep = ctx.enter_context(tc.tile_pool(name="keep", bufs=1))
+        h1p = ctx.enter_context(tc.tile_pool(name="h1p", bufs=3))
         stage = ctx.enter_context(tc.tile_pool(name="stage", bufs=2))
-        work = ctx.enter_context(tc.tile_pool(name="work", bufs=2))
+        batch = ctx.enter_context(tc.tile_pool(name="batch", bufs=2))
+        fft = ctx.enter_context(tc.tile_pool(name="fft", bufs=1))
         ps_tp = ctx.enter_context(tc.psum_pool(name="ps_tp", bufs=2))
-        ps_m1 = ctx.enter_context(tc.psum_pool(name="ps_m1", bufs=4))
+        ps_m1 = ctx.enter_context(tc.psum_pool(name="ps_m1", bufs=2))
         ps_m2 = ctx.enter_context(tc.psum_pool(name="ps_m2", bufs=1))
-        ps_y = ctx.enter_context(tc.psum_pool(name="ps_y", bufs=1))
+        ps_ms = ctx.enter_context(tc.psum_pool(name="ps_ms", bufs=3))
 
         w1_sb = keep.tile([P, 4, H], BF16)
         nc.sync.dma_start(out=w1_sb[:], in_=w_hid2.rearrange("(p c) k -> p c k", c=4))
-        h1_sb = keep.tile([P, TILES, H], BF16)
         h1_v = h1.rearrange("(p t) k -> p t k", t=TILES)
-        nc.sync.dma_start(out=h1_sb[:, 0:BLK, :], in_=h1_v[:, 0:BLK, :])
         w2_sb = keep.tile([P, H], BF16)
-        nc.sync.dma_start(out=w2_sb[:], in_=w_out)
         b1_bf = keep.tile([P, 4], BF16)
         b2_bf = keep.tile([P, 1], BF16)
         nr_bf = keep.tile([P, TILES], BF16)
@@ -49,19 +54,79 @@ def tile_qdtssolveronnx_pa_kernel(tc, h1, w_hid2, b_hid2, w_out, b_out, norm_roo
             nc.scalar.dma_start(out=b1_bf[:], in_=b_hid2.rearrange("(p c) -> p c", c=4))
             nc.scalar.dma_start(out=b2_bf[:], in_=b_out.rearrange("(p o) -> p o", o=1))
             nc.scalar.dma_start(out=nr_bf[:], in_=norm_root.rearrange("(p t) o -> p (t o)", t=TILES))
-        for i in range(1, NBLK):
-            nc.sync.dma_start(out=h1_sb[:, BLK * i:BLK * (i + 1), :], in_=h1_v[:, BLK * i:BLK * (i + 1), :])
-        t_sb = keep.tile([P, TILES, LAGS], BF16)
-        nc.sync.dma_start(out=t_sb[:], in_=T.rearrange("(p t) c -> p t c", t=TILES))
+        t_pad = keep.tile([P, TILES, N], BF16)
+        nc.vector.memset(t_pad[:], 0.0)
+
+        def sines(phase, width, name):
+            nc.vector.tensor_single_scalar(out=phase, in_=phase, scalar=511, op=ALU.bitwise_and)
+            ang = fft.tile([P, width], F32, name=name + "_ang", tag="m1")
+            nc.vector.tensor_scalar(out=ang[:], in0=phase, scalar1=-256.0, scalar2=None, op0=ALU.add)
+            edge = fft.tile([P, width], F32, name=name + "_edge", tag="m2")
+            nc.vector.tensor_scalar(out=edge[:], in0=ang[:], scalar1=-256.0, scalar2=256.0, op0=ALU.is_equal, op1=ALU.mult)
+            nc.vector.tensor_tensor(out=ang[:], in0=ang[:], in1=edge[:], op=ALU.add)
+            tab = keep.tile([P, width], F32, name=name + "_tab")
+            nc.scalar.activation(out=tab[:], in_=ang[:], func=AF.Sin, scale=math.pi / 256.0)
+            return tab
+
+        W_PRE = 2 * 2 * 2 * G
+        W_TW1 = 4 * 48
+        W_TW2 = 4 * 12
+        W_ALL = W_PRE + W_TW1 + W_TW2 + N
+        ph = keep.tile([P, W_ALL], I32)
+        for hf in range(2):
+            nc.gpsimd.iota(ph[:, 256 * hf:256 * (hf + 1)], pattern=[[64 + 256 * hf, 2], [128, 2], [1 + 4 * hf, G]],
+                           base=384, channel_multiplier=0)
+        tw1_ph = ph[:, W_PRE:W_PRE + W_TW1].rearrange("p (k j h) -> p k j h", k=4, h=3)
+        tw2_ph = ph[:, W_PRE + W_TW1:W_PRE + W_TW1 + W_TW2].rearrange("p (k j h) -> p k j h", k=4, h=3)
+        for hh in range(1, 4):
+            nc.gpsimd.iota(tw1_ph[:, :, :, hh - 1], pattern=[[128, 4], [8 * hh, 16]], base=384, channel_multiplier=0)
+            nc.gpsimd.iota(tw2_ph[:, :, :, hh - 1], pattern=[[128, 4], [32 * hh, 4]], base=384, channel_multiplier=0)
+        nc.gpsimd.iota(ph[:, W_ALL - N:W_ALL], pattern=[[-509, N]], base=LAGS * 509 + 384, channel_multiplier=0)
+        tabs = sines(ph[:], W_ALL, "row")
+        last_col = keep.tile([P, N], F32)
+        nc.vector.tensor_scalar(out=last_col[:], in0=tabs[:, W_ALL - N:W_ALL], scalar1=2.0, scalar2=None, op0=ALU.mult)
+        pre_tab = tabs[:, 0:W_PRE].rearrange("p (h a r n) -> p h a r n", h=2, a=2, r=2)
+        tw_tab = (tabs[:, W_PRE:W_PRE + W_TW1].rearrange("p (k c) -> p k c", k=4),
+                  tabs[:, W_PRE + W_TW1:W_PRE + W_TW1 + W_TW2].rearrange("p (k c) -> p k c", k=4))
+
+        pidx = keep.tile([P, 2], I32)
+        nc.gpsimd.iota(pidx[:, 0:1], pattern=[[0, 1]], base=0, channel_multiplier=1)
+        nc.gpsimd.iota(pidx[:, 1:2], pattern=[[0, 1]], base=LAGS, channel_multiplier=-1)
+        pf = keep.tile([P, 2], F32)
+        nc.vector.tensor_copy(out=pf[:], in_=pidx[:])
+        freq = keep.tile([P, 2, G], I32)
+        nc.gpsimd.iota(freq[:], pattern=[[4, 2], [8, G]], base=1, channel_multiplier=0)
+        mph = keep.tile([P, 4, G], I32)
+        nc.vector.tensor_scalar(out=mph[:, 0, :], in0=freq[:, 0, :], scalar1=pf[:, 0:1], scalar2=384.0, op0=ALU.mult, op1=ALU.add)
+        nc.vector.tensor_scalar(out=mph[:, 1, :], in0=freq[:, 0, :], scalar1=pf[:, 0:1], scalar2=256.0, op0=ALU.mult, op1=ALU.add)
+        nc.vector.tensor_scalar(out=mph[:, 2:4, :], in0=freq[:], scalar1=pf[:, 1:2], scalar2=384.0, op0=ALU.mult, op1=ALU.add)
+        mats = sines(mph[:].rearrange("p a g -> p (a g)"), 4 * G, "mat")
+        fx = mats[:, 0:2 * G]
+        ct = keep.tile([P, 2 * G], F32)
+        nc.vector.tensor_scalar(out=ct[:], in0=mats[:, 2 * G:4 * G], scalar1=2.0, scalar2=None, op0=ALU.mult)
 
         ident = keep.tile([P, P], F32)
         make_identity(nc, ident[:])
+        identb = keep.tile([P, P], BF16)
+        make_identity(nc, identb[:])
         b1 = keep.tile([P, 4], F32)
         nc.vector.tensor_copy(out=b1[:], in_=b1_bf[:])
         b2 = keep.tile([P, 1], F32)
         nc.vector.tensor_copy(out=b2[:], in_=b2_bf[:])
         nr = keep.tile([P, TILES], F32)
         nc.vector.tensor_copy(out=nr[:], in_=nr_bf[:])
+
+        h1_tiles = {}
+
+        def load_h1(i):
+            h1_sb = h1p.tile([P, BLK, H], BF16, name="h1_sb")
+            nc.sync.dma_start(out=h1_sb[:], in_=h1_v[:, BLK * i:BLK * (i + 1), :])
+            h1_tiles[i] = h1_sb
+
+        load_h1(0)
+        nc.sync.dma_start(out=w2_sb[:], in_=w_out)
+        load_h1(1)
+        nc.sync.dma_start(out=t_pad[:, :, 0:LAGS], in_=T.rearrange("(p t) c -> p t c", t=TILES))
 
         w1g = keep.tile([P, 4 * P, 4], BF16, align_bytes=64)
         w1g32 = w1g[:].bitcast(F32)
@@ -86,21 +151,37 @@ def tile_qdtssolveronnx_pa_kernel(tc, h1, w_hid2, b_hid2, w_out, b_out, norm_roo
         w2s = keep.tile([P, P], U8, align_bytes=64)
         nc.vector.quantize_mx(out=w2c[:].bitcast(FP8X4), scales=w2s[:], in_=w2g[:].rearrange("q n f -> q (n f)"))
 
-        xr = keep.tile([P, TILES, N], F32)
-        xc = keep.tile([P, TILES, N], F32)
         o0 = out_0.rearrange("(p t) j -> p t j", t=TILES)
         o2 = out_2.rearrange("(p t) j -> p t j", t=TILES)
-        h1_32 = h1_sb[:].bitcast(F32)
+        r0 = keep.tile([P, 2, TILES], F32)
+        acc_d = keep.tile([P, 2, NB], F32)
+        per_batch = {}
 
-        for i in range(NBLK):
+        def front(i):
+            b = [k for k, (first, cnt) in enumerate(BATCHES) if first <= i < first + cnt][0]
+            tb = BLK * BATCHES[b][1]
+            sub = slice(BLK * (i - BATCHES[b][0]), BLK * (i - BATCHES[b][0]) + BLK)
+            if b not in per_batch:
+                xq_new = batch.tile([P, 2, N, tb], F32, name="xq")
+                thq_new = batch.tile([P, 2, G, tb], F32, name="thq")
+                sq_new = batch.tile([P, 2, G, tb], F32, name="sq0")
+                per_batch[b] = (xq_new, thq_new, sq_new)
+            early = i == 0
+            xq, thq, sq0 = per_batch[b]
+            if i + 2 < NBLK:
+                load_h1(i + 2)
+            h1_32 = h1_tiles[i][:].bitcast(F32)
             h1g = stage.tile([P, BLK * P, 4], BF16, align_bytes=64)
             h1g32 = h1g[:].bitcast(F32)
             for a in range(2):
                 pt = ps_tp.tile([P, 2, 2, P], F32, tag="tp")
                 for u in range(2):
                     for tt in range(2):
-                        nc.tensor.transpose(pt[:, u, tt, :], h1_32[:, BLK * i + 2 * a + tt, P * u:P * (u + 1)], ident[:])
-                nc.scalar.copy(out=h1g32[:, 2 * P * a:2 * P * (a + 1), :], in_=pt[:].rearrange("q u t p -> q (t p) u"))
+                        nc.tensor.transpose(pt[:, u, tt, :], h1_32[:, 2 * a + tt, P * u:P * (u + 1)], ident[:])
+                if early:
+                    nc.vector.tensor_copy(out=h1g32[:, 2 * P * a:2 * P * (a + 1), :], in_=pt[:].rearrange("q u t p -> q (t p) u"))
+                else:
+                    nc.scalar.copy(out=h1g32[:, 2 * P * a:2 * P * (a + 1), :], in_=pt[:].rearrange("q u t p -> q (t p) u"))
             h1c = stage.tile([P, BLK * P], U32, align_bytes=64)
             h1s = stage.tile([P, BLK * P], U8, align_bytes=64)
             nc.vector.quantize_mx(out=h1c[:].bitcast(FP8X4), scales=h1s[:], in_=h1g[:].rearrange("q n f -> q (n f)"))
@@ -110,9 +191,15 @@ def tile_qdtssolveronnx_pa_kernel(tc, h1, w_hid2, b_hid2, w_out, b_out, norm_roo
                 p1 = ps_m1.tile([P, BLK * P], F32, tag="m1")
                 nc.tensor.matmul_mx(out=p1[:], lhsT=w1c[:, P * c:P * (c + 1)].bitcast(FP8X4), lhsT_scale=w1s[:, P * c:P * (c + 1)],
                                     rhs=h1c[:].bitcast(FP8X4), rhs_scale=h1s[:], start=True, stop=True)
-                nc.scalar.activation(out=h2p[:, c, :], in_=p1[:], func=AF.Relu, bias=b1[:, c:c + 1], scale=1.0)
+                if early and c % 2 == 1:
+                    nc.vector.tensor_scalar(out=h2p[:, c, :], in0=p1[:], scalar1=b1[:, c:c + 1], scalar2=0.0, op0=ALU.add, op1=ALU.max)
+                else:
+                    nc.scalar.activation(out=h2p[:, c, :], in_=p1[:], func=AF.Relu, bias=b1[:, c:c + 1], scale=1.0)
             h2g = stage.tile([P, BLK * P, 4], BF16, align_bytes=64)
-            nc.vector.tensor_copy(out=h2g[:], in_=h2p[:].rearrange("m c n -> m n c"))
+            if early:
+                nc.vector.tensor_copy(out=h2g[:], in_=h2p[:].rearrange("m c n -> m n c"))
+            else:
+                nc.scalar.copy(out=h2g[:], in_=h2p[:].rearrange("m c n -> m n c"))
             h2c = stage.tile([P, BLK * P], U32, align_bytes=64)
             h2s = stage.tile([P, BLK * P], U8, align_bytes=64)
             nc.vector.quantize_mx(out=h2c[:].bitcast(FP8X4), scales=h2s[:], in_=h2g[:].rearrange("m n f -> m (n f)"))
@@ -122,33 +209,166 @@ def tile_qdtssolveronnx_pa_kernel(tc, h1, w_hid2, b_hid2, w_out, b_out, norm_roo
                                 rhs=h2c[:].bitcast(FP8X4), rhs_scale=h2s[:], start=True, stop=True)
             yt = stage.tile([P, BLK * P], F32)
             nc.scalar.activation(out=yt[:], in_=p2[:], func=AF.Identity, bias=b2[:, 0:1], scale=1.0)
-            py = ps_y.tile([P, BLK, P], F32, tag="py")
+            py = ps_ms.tile([P, BLK, P], F32, tag="ms")
             for t in range(BLK):
                 nc.tensor.transpose(py[:, t, :], yt[:, P * t:P * (t + 1)], ident[:])
+            xr = stage.tile([P, BLK, N], F32)
+            xc = stage.tile([P, BLK, N], F32)
             for t in range(BLK):
                 g = BLK * i + t
-                nc.scalar.activation(out=xr[:, g, :], in_=py[:, t, :], func=AF.Copy, scale=nr[:, g:g + 1])
+                nc.scalar.activation(out=xr[:, t, :], in_=py[:, t, :], func=AF.Copy, scale=nr[:, g:g + 1])
+            nc.vector.tensor_scalar(out=xc[:], in0=xr[:], scalar1=-2.0, scalar2=2.0, op0=ALU.max, op1=ALU.min)
             blk = slice(BLK * i, BLK * (i + 1))
-            nc.gpsimd.tensor_scalar(out=xc[:, blk, :], in0=xr[:, blk, :], scalar1=-2.0, scalar2=2.0, op0=ALU.max, op1=ALU.min)
-            nc.sync.dma_start(out=o0[:, blk, :], in_=xr[:, blk, :])
-            nc.sync.dma_start(out=o2[:, blk, :], in_=xc[:, blk, :])
+            nc.sync.dma_start(out=o0[:, blk, :], in_=xr[:])
+            nc.sync.dma_start(out=o2[:, blk, :], in_=xc[:])
+            nc.scalar.copy(out=xq[:, 0, :, sub], in_=xr[:].rearrange("p t j -> p j t"))
+            nc.scalar.copy(out=xq[:, 1, :, sub], in_=xc[:].rearrange("p t j -> p j t"))
+
+            pxt = ps_ms.tile([P, BLK, P], F32, tag="ms")
+            for t in range(BLK):
+                nc.tensor.transpose(pxt[:, t, :], xr[:, t, :], ident[:])
+            xt = stage.tile([P, BLK, P], F32)
+            nc.scalar.copy(out=xt[:], in_=pxt[:])
+            pf0 = ps_ms.tile([P, BLK, P], F32, tag="ms")
+            for t in range(BLK):
+                nc.tensor.matmul(out=pf0[:, t, :], lhsT=xt[:, t, :], rhs=fx, start=True, stop=True)
+            nc.scalar.activation(out=sq0[:, :, :, sub].rearrange("p r g t -> p (r g) t"), in_=pf0[:].rearrange("p t c -> p c t"),
+                                 func=AF.Square)
+            ptt = ps_ms.tile([P, BLK, P], BF16, tag="ms")
+            for t in range(BLK):
+                nc.tensor.transpose(ptt[:, t, :], t_pad[:, BLK * i + t, :], identb[:])
+            ttr = stage.tile([P, BLK, P], F32)
+            nc.scalar.copy(out=ttr[:], in_=ptt[:])
+            pth = ps_ms.tile([P, BLK, P], F32, tag="ms")
+            for t in range(BLK):
+                if BLK * i + t == TILES - 1:
+                    nc.tensor.transpose(pth[:, t, :], ttr[:, t, :], ident[:])
+                    nc.tensor.matmul(out=pth[:, t, 0:P - 1], lhsT=ttr[:, t, :], rhs=ct[:, 0:P - 1], start=True, stop=True)
+                else:
+                    nc.tensor.matmul(out=pth[:, t, :], lhsT=ttr[:, t, :], rhs=ct[:], start=True, stop=True)
+            nc.scalar.copy(out=thq[:, :, :, sub].rearrange("p h g t -> p (h g) t"), in_=pth[:].rearrange("p t c -> p c t"))
+            if i == NBLK - 1:
+                fix = stage.tile([P, N], F32)
+                nc.vector.tensor_tensor(out=fix[:], in0=t_pad[:, TILES - 1, :], in1=last_col[:], op=ALU.mult)
+                nc.vector.tensor_reduce(out=thq[:, 1, G - 1, tb - 1:tb], in_=fix[:], axis=AX.X, op=ALU.add)
+
+            junk = stage.tile([P, N], F32)
+            for t in range(BLK):
+                g = BLK * i + t
+                nc.scalar.activation(out=junk[:], in_=xr[:, t, :], func=AF.Square, accum_out=r0[:, 0, g:g + 1])
+                nc.scalar.activation(out=junk[:], in_=xc[:, t, :], func=AF.Square, accum_out=r0[:, 1, g:g + 1])
+
+        TT = nc.vector.tensor_tensor
+
+        started = {}
+
+        def twist(b):
+            xq, thq, sq0 = per_batch[b]
+            TB = BLK * BATCHES[b][1]
+            Q = 3 * TB
+            cur = fft.tile([P, 2, G * Q], F32, tag="va")
+            started[b] = cur
+            cur_v = cur[:].rearrange("p r (n s t) -> p r n s t", s=3, t=TB)
+            for s3, (sig, hf) in enumerate(((0, 1), (1, 0), (1, 1))):
+                u1 = fft.tile([P, 2, G, TB], F32, tag="m1")
+                u2 = fft.tile([P, 2, G, TB], F32, tag="m2")
+                shape = [P, 2, G, TB]
+                TT(out=u1[:], in0=xq[:, sig, 0:G, :].unsqueeze(1).to_broadcast(shape),
+                   in1=pre_tab[:, hf, 0, :, :].unsqueeze(3).to_broadcast(shape), op=ALU.mult)
+                TT(out=u2[:], in0=xq[:, sig, G:N, :].unsqueeze(1).to_broadcast(shape),
+                   in1=pre_tab[:, hf, 1, :, :].unsqueeze(3).to_broadcast(shape), op=ALU.mult)
+                TT(out=cur_v[:, :, :, s3, :], in0=u1[:], in1=u2[:], op=ALU.add)
+
+        def stages(b):
+            TB = BLK * BATCHES[b][1]
+            Q = 3 * TB
+            cur = started[b]
+            for st, (l, m) in enumerate(((16, 1), (4, 4), (1, 16))):
+                x4 = 16 * Q
+                y = m * Q
+                xin = cur[:].rearrange("p r (h x) -> p r h x", h=4)
+                sm = fft.tile([P, 2, 2 * x4], F32, tag="sm")
+                df = fft.tile([P, 2, 2 * x4], F32, tag="df")
+                TT(out=sm[:].rearrange("p r (a x) -> p r a x", a=2), in0=xin[:, :, 0:2, :], in1=xin[:, :, 2:4, :], op=ALU.add)
+                TT(out=df[:].rearrange("p r (a x) -> p r a x", a=2), in0=xin[:, :, 0:2, :], in1=xin[:, :, 2:4, :], op=ALU.subtract)
+                sm5 = sm[:].rearrange("p r (a j y) -> p r a j y", a=2, j=l)
+                df5 = df[:].rearrange("p r (a j y) -> p r a j y", a=2, j=l)
+                nxt = fft.tile([P, 2, G * Q], F32, tag=("vb", "va", "vb")[st])
+                nxt_v = nxt[:].rearrange("p r (j h y) -> p r j h y", j=l, h=4)
+                TT(out=nxt_v[:, :, :, 0, :], in0=sm5[:, :, 0, :, :], in1=sm5[:, :, 1, :, :], op=ALU.add)
+                if l > 1:
+                    y3 = fft.tile([P, 2, 3 * x4], F32, tag="y3")
+                    o3 = y3[:].rearrange("p r (j h y) -> p r j h y", j=l, h=3)
+                    off = 0
+                else:
+                    o3 = nxt_v
+                    off = 1
+                TT(out=o3[:, :, :, off + 1, :], in0=sm5[:, :, 0, :, :], in1=sm5[:, :, 1, :, :], op=ALU.subtract)
+                TT(out=o3[:, 0, :, off, :], in0=df5[:, 0, 0, :, :], in1=df5[:, 1, 1, :, :], op=ALU.add)
+                TT(out=o3[:, 1, :, off, :], in0=df5[:, 1, 0, :, :], in1=df5[:, 0, 1, :, :], op=ALU.subtract)
+                TT(out=o3[:, 0, :, off + 2, :], in0=df5[:, 0, 0, :, :], in1=df5[:, 1, 1, :, :], op=ALU.subtract)
+                TT(out=o3[:, 1, :, off + 2, :], in0=df5[:, 1, 0, :, :], in1=df5[:, 0, 1, :, :], op=ALU.add)
+                if l > 1:
+                    tw = tw_tab[st]
+                    shape = [P, 2, 3 * l, y]
+                    y3c = y3[:].rearrange("p r (c y) -> p r c y", c=3 * l)
+                    m1 = fft.tile([P, 2, 3 * x4], F32, tag="m1")
+                    m2 = fft.tile([P, 2, 3 * x4], F32, tag="m2")
+                    TT(out=m1[:].rearrange("p r (c y) -> p r c y", c=3 * l), in0=y3c,
+                       in1=tw[:, 0:1, :].unsqueeze(3).to_broadcast(shape), op=ALU.mult)
+                    TT(out=m2[:].rearrange("p r (c y) -> p r c y", c=3 * l), in0=y3c,
+                       in1=tw.rearrange("p (a b) c -> p a b c", b=2)[:, :, 1, :].unsqueeze(3).to_broadcast(shape), op=ALU.mult)
+                    m1v = m1[:].rearrange("p r (j z) -> p r j z", j=l)
+                    m2v = m2[:].rearrange("p r (j z) -> p r j z", j=l)
+                    nz = nxt[:].rearrange("p r (j z) -> p r j z", j=l)
+                    TT(out=nz[:, 0, :, y:4 * y], in0=m1v[:, 0, :, :], in1=m2v[:, 1, :, :], op=ALU.add)
+                    TT(out=nz[:, 1, :, y:4 * y], in0=m1v[:, 1, :, :], in1=m2v[:, 0, :, :], op=ALU.add)
+                cur = nxt
+            sq3 = fft.tile([P, 2, G, 3, TB], F32, tag="sq3")
+            nc.scalar.activation(out=sq3[:].rearrange("p r g s t -> p r (g s t)"), in_=cur[:], func=AF.Square)
+            started[b] = sq3
+
+        def finish(b):
+            xq, thq, sq0 = per_batch[b]
+            TB = BLK * BATCHES[b][1]
+            sq3 = started[b]
+            pw = fft.tile([P, G, 4, TB], F32, tag="pw")
+            TT(out=pw[:, :, 0, :], in0=sq0[:, 0, :, :], in1=sq0[:, 1, :, :], op=ALU.add)
+            TT(out=pw[:, :, 1:4, :], in0=sq3[:, 0, :, :, :], in1=sq3[:, 1, :, :, :], op=ALU.add)
+            dd = fft.tile([P, G, 4, TB], F32, tag="dd")
+            thv = thq[:].rearrange("p h g t -> p g h t")
+            for sig in range(2):
+                TT(out=dd[:, :, 2 * sig:2 * sig + 2, :], in0=pw[:, :, 2 * sig:2 * sig + 2, :], in1=thv, op=ALU.subtract)
+            for sig in range(2):
+                d2 = fft.tile([P, G, 2, TB], F32, tag="d2")
+                nc.scalar.activation(out=d2[:], in_=dd[:, :, 2 * sig:2 * sig + 2, :], func=AF.Square, accum_out=acc_d[:, sig, b:b + 1])
+
+        for i in range(BATCHES[2][0]):
+            front(i)
+        twist(0)
+        for b in range(NB):
+            stages(b)
+            if b + 1 < NB:
+                twist(b + 1)
+            finish(b)
+            if b + 2 < NB:
+                for i in range(BATCHES[b + 2][0], BATCHES[b + 2][0] + BATCHES[b + 2][1]):
+                    front(i)
 
         sums = keep.tile([P, P], F32)
         nc.vector.memset(sums[:], 0.0)
-        for s, sig in enumerate((xr, xc)):
-            z = work.tile([P, TILES, LAGS], F32, tag="z")
-            for k in range(1, N):
-                prod = work.tile([P, TILES, LAGS], F32, tag="prod")
-                nc.vector.tensor_tensor(out=prod[:, :, 0:N - k], in0=sig[:, :, 0:N - k], in1=sig[:, :, k:N], op=ALU.mult)
-                nc.vector.tensor_reduce(out=z[:, :, LAGS - k:LAGS - k + 1], in_=prod[:, :, 0:N - k], axis=AX.X, op=ALU.add)
-            nc.vector.tensor_tensor(out=z[:], in0=z[:], in1=t_sb[:], op=ALU.subtract)
-            sq = work.tile([P, TILES, LAGS], F32, tag="prod")
-            nc.scalar.activation(out=sq[:], in_=z[:], func=AF.Square, accum_out=sums[:, s:s + 1])
-        pf = ps_y.tile([P, P], F32, tag="py")
-        nc.tensor.transpose(pf[:], sums[:], ident[:])
+        acc_r = keep.tile([P, 2], F32)
+        junk2 = keep.tile([P, TILES], F32)
+        for sig in range(2):
+            nc.scalar.activation(out=junk2[:], in_=r0[:, sig, :], func=AF.Square, accum_out=acc_r[:, sig:sig + 1])
+        sum_d = keep.tile([P, 2], F32)
+        nc.vector.tensor_reduce(out=sum_d[:], in_=acc_d[:], axis=AX.X, op=ALU.add)
+        nc.vector.scalar_tensor_tensor(out=sums[:, 0:2], in0=sum_d[:], scalar=1.0 / 128.0, in1=acc_r[:], op0=ALU.mult, op1=ALU.subtract)
+        pfin = ps_ms.tile([P, P], F32, tag="ms")
+        nc.tensor.transpose(pfin[:], sums[:], ident[:])
         tot = keep.tile([P, 1], F32)
-        nc.vector.tensor_reduce(out=tot[:], in_=pf[:], axis=AX.X, op=ALU.add)
+        nc.vector.tensor_reduce(out=tot[:], in_=pfin[:], axis=AX.X, op=ALU.add)
         res = keep.tile([P, 1], F32)
-        nc.vector.tensor_scalar(out=res[:], in0=tot[:], scalar1=1.0 / (B * LAGS), scalar2=None, op0=ALU.mult)
+        nc.vector.tensor_scalar(out=res[:], in0=tot[:], scalar1=1.0 / (2.0 * B * LAGS), scalar2=None, op0=ALU.mult)
         nc.sync.dma_start(out=out_1.rearrange("(a b) -> a b", a=1), in_=res[0:1, 0:1])
         nc.sync.dma_start(out=out_3.rearrange("(a b) -> a b", a=1), in_=res[1:2, 0:1])

@@ -38,10 +38,11 @@ def tile_qdtssolveronnx_pa_kernel(tc, h1, w_hid2, b_hid2, w_out, b_out, norm_roo
         stage = ctx.enter_context(tc.tile_pool(name="stage", bufs=2))
         batch = ctx.enter_context(tc.tile_pool(name="batch", bufs=2))
         fft = ctx.enter_context(tc.tile_pool(name="fft", bufs=1))
-        ps_tp = ctx.enter_context(tc.psum_pool(name="ps_tp", bufs=2))
+        zpool = ctx.enter_context(tc.tile_pool(name="zpool", bufs=3))
+        ps_tp = ctx.enter_context(tc.psum_pool(name="ps_tp", bufs=1))
         ps_m1 = ctx.enter_context(tc.psum_pool(name="ps_m1", bufs=2))
         ps_m2 = ctx.enter_context(tc.psum_pool(name="ps_m2", bufs=1))
-        ps_ms = ctx.enter_context(tc.psum_pool(name="ps_ms", bufs=3))
+        psum = ctx.enter_context(tc.psum_pool(name="psum", bufs=4))
 
         w1_sb = keep.tile([P, 4, H], BF16)
         nc.sync.dma_start(out=w1_sb[:], in_=w_hid2.rearrange("(p c) k -> p c k", c=4))
@@ -68,14 +69,11 @@ def tile_qdtssolveronnx_pa_kernel(tc, h1, w_hid2, b_hid2, w_out, b_out, norm_roo
             nc.scalar.activation(out=tab[:], in_=ang[:], func=AF.Sin, scale=math.pi / 256.0)
             return tab
 
-        W_PRE = 2 * 2 * 2 * G
+        W_PRE = 0
         W_TW1 = 4 * 48
         W_TW2 = 4 * 12
         W_ALL = W_PRE + W_TW1 + W_TW2 + N
         ph = keep.tile([P, W_ALL], I32)
-        for hf in range(2):
-            nc.gpsimd.iota(ph[:, 256 * hf:256 * (hf + 1)], pattern=[[64 + 256 * hf, 2], [128, 2], [1 + 4 * hf, G]],
-                           base=384, channel_multiplier=0)
         tw1_ph = ph[:, W_PRE:W_PRE + W_TW1].rearrange("p (k j h) -> p k j h", k=4, h=3)
         tw2_ph = ph[:, W_PRE + W_TW1:W_PRE + W_TW1 + W_TW2].rearrange("p (k j h) -> p k j h", k=4, h=3)
         for hh in range(1, 4):
@@ -85,7 +83,6 @@ def tile_qdtssolveronnx_pa_kernel(tc, h1, w_hid2, b_hid2, w_out, b_out, norm_roo
         tabs = sines(ph[:], W_ALL, "row")
         last_col = keep.tile([P, N], F32)
         nc.vector.tensor_scalar(out=last_col[:], in0=tabs[:, W_ALL - N:W_ALL], scalar1=2.0, scalar2=None, op0=ALU.mult)
-        pre_tab = tabs[:, 0:W_PRE].rearrange("p (h a r n) -> p h a r n", h=2, a=2, r=2)
         tw_tab = (tabs[:, W_PRE:W_PRE + W_TW1].rearrange("p (k c) -> p k c", k=4),
                   tabs[:, W_PRE + W_TW1:W_PRE + W_TW1 + W_TW2].rearrange("p (k c) -> p k c", k=4))
 
@@ -96,11 +93,14 @@ def tile_qdtssolveronnx_pa_kernel(tc, h1, w_hid2, b_hid2, w_out, b_out, norm_roo
         nc.vector.tensor_copy(out=pf[:], in_=pidx[:])
         freq = keep.tile([P, 2, G], I32)
         nc.gpsimd.iota(freq[:], pattern=[[4, 2], [8, G]], base=1, channel_multiplier=0)
-        mph = keep.tile([P, 4, G], I32)
-        nc.vector.tensor_scalar(out=mph[:, 0, :], in0=freq[:, 0, :], scalar1=pf[:, 0:1], scalar2=384.0, op0=ALU.mult, op1=ALU.add)
-        nc.vector.tensor_scalar(out=mph[:, 1, :], in0=freq[:, 0, :], scalar1=pf[:, 0:1], scalar2=256.0, op0=ALU.mult, op1=ALU.add)
-        nc.vector.tensor_scalar(out=mph[:, 2:4, :], in0=freq[:], scalar1=pf[:, 1:2], scalar2=384.0, op0=ALU.mult, op1=ALU.add)
-        mats = sines(mph[:].rearrange("p a g -> p (a g)"), 4 * G, "mat")
+        mph = keep.tile([P, 4 * G + 4], I32)
+        for hf in range(2):
+            nc.gpsimd.iota(mph[:, 4 * G + 2 * hf:4 * G + 2 * hf + 2], pattern=[[128, 2]], base=384, channel_multiplier=1 + 4 * hf)
+        nc.vector.tensor_scalar(out=mph[:, 0:G], in0=freq[:, 0, :], scalar1=pf[:, 0:1], scalar2=384.0, op0=ALU.mult, op1=ALU.add)
+        nc.vector.tensor_scalar(out=mph[:, G:2 * G], in0=freq[:, 0, :], scalar1=pf[:, 0:1], scalar2=256.0, op0=ALU.mult, op1=ALU.add)
+        nc.vector.tensor_scalar(out=mph[:, 2 * G:4 * G], in0=freq[:].rearrange("p h g -> p (h g)"), scalar1=pf[:, 1:2], scalar2=384.0, op0=ALU.mult, op1=ALU.add)
+        mats = sines(mph[:], 4 * G + 4, "mat")
+        cvec = mats[:, 4 * G:4 * G + 4]
         fx = mats[:, 0:2 * G]
         ct = keep.tile([P, 2 * G], F32)
         nc.vector.tensor_scalar(out=ct[:], in0=mats[:, 2 * G:4 * G], scalar1=2.0, scalar2=None, op0=ALU.mult)
@@ -162,12 +162,13 @@ def tile_qdtssolveronnx_pa_kernel(tc, h1, w_hid2, b_hid2, w_out, b_out, norm_roo
             tb = BLK * BATCHES[b][1]
             sub = slice(BLK * (i - BATCHES[b][0]), BLK * (i - BATCHES[b][0]) + BLK)
             if b not in per_batch:
-                xq_new = batch.tile([P, 2, N, tb], F32, name="xq")
+                xq_new = batch.tile([P, 2, G * 3 * tb], F32, name="vin")
                 thq_new = batch.tile([P, 2, G, tb], F32, name="thq")
                 sq_new = batch.tile([P, 2, G, tb], F32, name="sq0")
                 per_batch[b] = (xq_new, thq_new, sq_new)
-            early = i == 0
-            xq, thq, sq0 = per_batch[b]
+            early = i <= 2
+            vin, thq, sq0 = per_batch[b]
+            vin_v = vin[:].rearrange("p r (n s t) -> p r n s t", s=3, t=tb)
             if i + 2 < NBLK:
                 load_h1(i + 2)
             h1_32 = h1_tiles[i][:].bitcast(F32)
@@ -209,7 +210,7 @@ def tile_qdtssolveronnx_pa_kernel(tc, h1, w_hid2, b_hid2, w_out, b_out, norm_roo
                                 rhs=h2c[:].bitcast(FP8X4), rhs_scale=h2s[:], start=True, stop=True)
             yt = stage.tile([P, BLK * P], F32)
             nc.scalar.activation(out=yt[:], in_=p2[:], func=AF.Identity, bias=b2[:, 0:1], scale=1.0)
-            py = ps_ms.tile([P, BLK, P], F32, tag="ms")
+            py = ps_m2.tile([P, BLK, P], F32, tag="m2")
             for t in range(BLK):
                 nc.tensor.transpose(py[:, t, :], yt[:, P * t:P * (t + 1)], ident[:])
             xr = stage.tile([P, BLK, N], F32)
@@ -221,25 +222,36 @@ def tile_qdtssolveronnx_pa_kernel(tc, h1, w_hid2, b_hid2, w_out, b_out, norm_roo
             blk = slice(BLK * i, BLK * (i + 1))
             nc.sync.dma_start(out=o0[:, blk, :], in_=xr[:])
             nc.sync.dma_start(out=o2[:, blk, :], in_=xc[:])
-            nc.scalar.copy(out=xq[:, 0, :, sub], in_=xr[:].rearrange("p t j -> p j t"))
-            nc.scalar.copy(out=xq[:, 1, :, sub], in_=xc[:].rearrange("p t j -> p j t"))
 
-            pxt = ps_ms.tile([P, BLK, P], F32, tag="ms")
+            pxt = psum.tile([P, BLK, P], F32, tag="ps")
             for t in range(BLK):
                 nc.tensor.transpose(pxt[:, t, :], xr[:, t, :], ident[:])
             xt = stage.tile([P, BLK, P], F32)
             nc.scalar.copy(out=xt[:], in_=pxt[:])
-            pf0 = ps_ms.tile([P, BLK, P], F32, tag="ms")
+            pxc = psum.tile([P, BLK, P], F32, tag="ps")
+            for t in range(BLK):
+                nc.tensor.transpose(pxc[:, t, :], xc[:, t, :], ident[:])
+            for s3, (src, hf) in enumerate(((pxt, 1), (pxc, 0), (pxc, 1))):
+                for r in range(2):
+                    zt = zpool.tile([P, BLK, P], F32, name="zt")
+                    nc.scalar.activation(out=zt[:], in_=src[:], func=AF.Copy, scale=cvec[:, 2 * hf + r:2 * hf + r + 1])
+                    pv = psum.tile([P, BLK, P], F32, tag="ps")
+                    for t in range(BLK):
+                        nc.tensor.transpose(pv[:, t, :], zt[:, t, :], ident[:])
+                    up = zpool.tile([P, G, BLK], F32, name="up")
+                    nc.scalar.copy(out=up[:], in_=pv[:, :, G:N].rearrange("p t n -> p n t"))
+                    nc.vector.tensor_tensor(out=vin_v[:, r, :, s3, sub], in0=pv[:, :, 0:G].rearrange("p t n -> p n t"), in1=up[:], op=ALU.add)
+            pf0 = psum.tile([P, BLK, P], F32, tag="ps")
             for t in range(BLK):
                 nc.tensor.matmul(out=pf0[:, t, :], lhsT=xt[:, t, :], rhs=fx, start=True, stop=True)
             nc.scalar.activation(out=sq0[:, :, :, sub].rearrange("p r g t -> p (r g) t"), in_=pf0[:].rearrange("p t c -> p c t"),
                                  func=AF.Square)
-            ptt = ps_ms.tile([P, BLK, P], BF16, tag="ms")
+            ptt = psum.tile([P, BLK, P], BF16, tag="ps")
             for t in range(BLK):
                 nc.tensor.transpose(ptt[:, t, :], t_pad[:, BLK * i + t, :], identb[:])
             ttr = stage.tile([P, BLK, P], F32)
             nc.scalar.copy(out=ttr[:], in_=ptt[:])
-            pth = ps_ms.tile([P, BLK, P], F32, tag="ms")
+            pth = psum.tile([P, BLK, P], F32, tag="ps")
             for t in range(BLK):
                 if BLK * i + t == TILES - 1:
                     nc.tensor.transpose(pth[:, t, :], ttr[:, t, :], ident[:])
@@ -262,27 +274,10 @@ def tile_qdtssolveronnx_pa_kernel(tc, h1, w_hid2, b_hid2, w_out, b_out, norm_roo
 
         started = {}
 
-        def twist(b):
-            xq, thq, sq0 = per_batch[b]
-            TB = BLK * BATCHES[b][1]
-            Q = 3 * TB
-            cur = fft.tile([P, 2, G * Q], F32, tag="va")
-            started[b] = cur
-            cur_v = cur[:].rearrange("p r (n s t) -> p r n s t", s=3, t=TB)
-            for s3, (sig, hf) in enumerate(((0, 1), (1, 0), (1, 1))):
-                u1 = fft.tile([P, 2, G, TB], F32, tag="m1")
-                u2 = fft.tile([P, 2, G, TB], F32, tag="m2")
-                shape = [P, 2, G, TB]
-                TT(out=u1[:], in0=xq[:, sig, 0:G, :].unsqueeze(1).to_broadcast(shape),
-                   in1=pre_tab[:, hf, 0, :, :].unsqueeze(3).to_broadcast(shape), op=ALU.mult)
-                TT(out=u2[:], in0=xq[:, sig, G:N, :].unsqueeze(1).to_broadcast(shape),
-                   in1=pre_tab[:, hf, 1, :, :].unsqueeze(3).to_broadcast(shape), op=ALU.mult)
-                TT(out=cur_v[:, :, :, s3, :], in0=u1[:], in1=u2[:], op=ALU.add)
-
         def stages(b):
             TB = BLK * BATCHES[b][1]
             Q = 3 * TB
-            cur = started[b]
+            cur = per_batch[b][0]
             for st, (l, m) in enumerate(((16, 1), (4, 4), (1, 16))):
                 x4 = 16 * Q
                 y = m * Q
@@ -324,32 +319,32 @@ def tile_qdtssolveronnx_pa_kernel(tc, h1, w_hid2, b_hid2, w_out, b_out, norm_roo
                     TT(out=nz[:, 0, :, y:4 * y], in0=m1v[:, 0, :, :], in1=m2v[:, 1, :, :], op=ALU.add)
                     TT(out=nz[:, 1, :, y:4 * y], in0=m1v[:, 1, :, :], in1=m2v[:, 0, :, :], op=ALU.add)
                 cur = nxt
-            sq3 = fft.tile([P, 2, G, 3, TB], F32, tag="sq3")
-            nc.scalar.activation(out=sq3[:].rearrange("p r g s t -> p r (g s t)"), in_=cur[:], func=AF.Square)
-            started[b] = sq3
+            fin = cur[:].rearrange("p r (h y) -> p r h y", h=4)
+            for hb in (0, 2, 1, 3):
+                nc.scalar.activation(out=fin[:, :, hb, :], in_=fin[:, :, hb, :], func=AF.Square)
+            started[b] = cur
 
         def finish(b):
-            xq, thq, sq0 = per_batch[b]
+            vin, thq, sq0 = per_batch[b]
             TB = BLK * BATCHES[b][1]
-            sq3 = started[b]
+            sqv = started[b][:].rearrange("p r (g s t) -> p r g s t", s=3, t=TB)
             pw = fft.tile([P, G, 4, TB], F32, tag="pw")
             TT(out=pw[:, :, 0, :], in0=sq0[:, 0, :, :], in1=sq0[:, 1, :, :], op=ALU.add)
-            TT(out=pw[:, :, 1:4, :], in0=sq3[:, 0, :, :, :], in1=sq3[:, 1, :, :, :], op=ALU.add)
-            dd = fft.tile([P, G, 4, TB], F32, tag="dd")
+            for hb in (0, 2, 1, 3):
+                gs = slice(16 * hb, 16 * hb + 16)
+                TT(out=pw[:, gs, 1:4, :], in0=sqv[:, 0, gs, :, :], in1=sqv[:, 1, gs, :, :], op=ALU.add)
             thv = thq[:].rearrange("p h g t -> p g h t")
             for sig in range(2):
-                TT(out=dd[:, :, 2 * sig:2 * sig + 2, :], in0=pw[:, :, 2 * sig:2 * sig + 2, :], in1=thv, op=ALU.subtract)
+                half = pw[:, :, 2 * sig:2 * sig + 2, :]
+                TT(out=half, in0=half, in1=thv, op=ALU.subtract)
             for sig in range(2):
-                d2 = fft.tile([P, G, 2, TB], F32, tag="d2")
-                nc.scalar.activation(out=d2[:], in_=dd[:, :, 2 * sig:2 * sig + 2, :], func=AF.Square, accum_out=acc_d[:, sig, b:b + 1])
+                half = pw[:, :, 2 * sig:2 * sig + 2, :]
+                nc.scalar.activation(out=half, in_=half, func=AF.Square, accum_out=acc_d[:, sig, b:b + 1])
 
         for i in range(BATCHES[2][0]):
             front(i)
-        twist(0)
         for b in range(NB):
             stages(b)
-            if b + 1 < NB:
-                twist(b + 1)
             finish(b)
             if b + 2 < NB:
                 for i in range(BATCHES[b + 2][0], BATCHES[b + 2][0] + BATCHES[b + 2][1]):
@@ -364,7 +359,7 @@ def tile_qdtssolveronnx_pa_kernel(tc, h1, w_hid2, b_hid2, w_out, b_out, norm_roo
         sum_d = keep.tile([P, 2], F32)
         nc.vector.tensor_reduce(out=sum_d[:], in_=acc_d[:], axis=AX.X, op=ALU.add)
         nc.vector.scalar_tensor_tensor(out=sums[:, 0:2], in0=sum_d[:], scalar=1.0 / 128.0, in1=acc_r[:], op0=ALU.mult, op1=ALU.subtract)
-        pfin = ps_ms.tile([P, P], F32, tag="ms")
+        pfin = psum.tile([P, P], F32, tag="ps")
         nc.tensor.transpose(pfin[:], sums[:], ident[:])
         tot = keep.tile([P, 1], F32)
         nc.vector.tensor_reduce(out=tot[:], in_=pfin[:], axis=AX.X, op=ALU.add)

@@ -26,6 +26,7 @@ BATCHES = ((0, 1), (1, 2), (3, 2), (5, 2), (7, 1))
 NB = len(BATCHES)
 TBMAX = 8
 G = 64
+GROUPS = ((0, 2), (1, 4), (3, 4))
 
 FLOPS = 2 * B * H * (H + N) + 2 * 2 * B * (N * LAGS // 2)
 
@@ -60,7 +61,7 @@ def tile_qdtssolveronnx_pa_kernel(tc, h1, w_hid2, b_hid2, w_out, b_out, norm_roo
 
         def sines(phase, width, name):
             nc.vector.tensor_single_scalar(out=phase, in_=phase, scalar=511, op=ALU.bitwise_and)
-            ang = fft.tile([P, width], F32, name=name + "_ang", tag="m1")
+            ang = fft.tile([P, width], F32, name=name + "_ang", tag="y7")
             nc.vector.tensor_scalar(out=ang[:], in0=phase, scalar1=-256.0, scalar2=None, op0=ALU.add)
             edge = fft.tile([P, width], F32, name=name + "_edge", tag="m2")
             nc.vector.tensor_scalar(out=edge[:], in0=ang[:], scalar1=-256.0, scalar2=256.0, op0=ALU.is_equal, op1=ALU.mult)
@@ -69,22 +70,17 @@ def tile_qdtssolveronnx_pa_kernel(tc, h1, w_hid2, b_hid2, w_out, b_out, norm_roo
             nc.scalar.activation(out=tab[:], in_=ang[:], func=AF.Sin, scale=math.pi / 256.0)
             return tab
 
-        W_PRE = 0
-        W_TW1 = 4 * 48
-        W_TW2 = 4 * 12
-        W_ALL = W_PRE + W_TW1 + W_TW2 + N
+        W_TW = 4 * 56
+        W_ALL = W_TW + N
         ph = keep.tile([P, W_ALL], I32)
-        tw1_ph = ph[:, W_PRE:W_PRE + W_TW1].rearrange("p (k j h) -> p k j h", k=4, h=3)
-        tw2_ph = ph[:, W_PRE + W_TW1:W_PRE + W_TW1 + W_TW2].rearrange("p (k j h) -> p k j h", k=4, h=3)
-        for hh in range(1, 4):
-            nc.gpsimd.iota(tw1_ph[:, :, :, hh - 1], pattern=[[128, 4], [8 * hh, 16]], base=384, channel_multiplier=0)
-            nc.gpsimd.iota(tw2_ph[:, :, :, hh - 1], pattern=[[128, 4], [32 * hh, 4]], base=384, channel_multiplier=0)
+        tw_ph = ph[:, 0:W_TW].rearrange("p (k j h) -> p k j h", k=4, h=7)
+        for hh in range(1, 8):
+            nc.gpsimd.iota(tw_ph[:, :, :, hh - 1], pattern=[[128, 4], [8 * hh, 8]], base=384, channel_multiplier=0)
         nc.gpsimd.iota(ph[:, W_ALL - N:W_ALL], pattern=[[-509, N]], base=LAGS * 509 + 384, channel_multiplier=0)
         tabs = sines(ph[:], W_ALL, "row")
         last_col = keep.tile([P, N], F32)
         nc.vector.tensor_scalar(out=last_col[:], in0=tabs[:, W_ALL - N:W_ALL], scalar1=2.0, scalar2=None, op0=ALU.mult)
-        tw_tab = (tabs[:, W_PRE:W_PRE + W_TW1].rearrange("p (k c) -> p k c", k=4),
-                  tabs[:, W_PRE + W_TW1:W_PRE + W_TW1 + W_TW2].rearrange("p (k c) -> p k c", k=4))
+        tw = tabs[:, 0:W_TW].rearrange("p (k c) -> p k c", k=4)
 
         pidx = keep.tile([P, 2], I32)
         nc.gpsimd.iota(pidx[:, 0:1], pattern=[[0, 1]], base=0, channel_multiplier=1)
@@ -197,10 +193,12 @@ def tile_qdtssolveronnx_pa_kernel(tc, h1, w_hid2, b_hid2, w_out, b_out, norm_roo
                 else:
                     nc.scalar.activation(out=h2p[:, c, :], in_=p1[:], func=AF.Relu, bias=b1[:, c:c + 1], scale=1.0)
             h2g = stage.tile([P, BLK * P, 4], BF16, align_bytes=64)
+            h2g_runs = h2g[:].rearrange("m (a i) c -> m a c i", i=4)
+            h2p_runs = h2p[:].rearrange("m c (a i) -> m a c i", i=4)
             if early:
-                nc.vector.tensor_copy(out=h2g[:], in_=h2p[:].rearrange("m c n -> m n c"))
+                nc.vector.tensor_copy(out=h2g_runs, in_=h2p_runs)
             else:
-                nc.scalar.copy(out=h2g[:], in_=h2p[:].rearrange("m c n -> m n c"))
+                nc.scalar.copy(out=h2g_runs, in_=h2p_runs)
             h2c = stage.tile([P, BLK * P], U32, align_bytes=64)
             h2s = stage.tile([P, BLK * P], U8, align_bytes=64)
             nc.vector.quantize_mx(out=h2c[:].bitcast(FP8X4), scales=h2s[:], in_=h2g[:].rearrange("m n f -> m (n f)"))
@@ -272,67 +270,102 @@ def tile_qdtssolveronnx_pa_kernel(tc, h1, w_hid2, b_hid2, w_out, b_out, norm_roo
 
         TT = nc.vector.tensor_tensor
 
-        started = {}
+        STT = nc.vector.scalar_tensor_tensor
+        RHO = math.sqrt(0.5)
 
         def stages(b):
             TB = BLK * BATCHES[b][1]
             Q = 3 * TB
-            cur = per_batch[b][0]
-            for st, (l, m) in enumerate(((16, 1), (4, 4), (1, 16))):
-                x4 = 16 * Q
+            x8 = 8 * Q
+            vin = per_batch[b][0]
+            cur = vin
+            for l, m in ((8, 1), (1, 8)):
                 y = m * Q
-                xin = cur[:].rearrange("p r (h x) -> p r h x", h=4)
-                sm = fft.tile([P, 2, 2 * x4], F32, tag="sm")
-                df = fft.tile([P, 2, 2 * x4], F32, tag="df")
-                TT(out=sm[:].rearrange("p r (a x) -> p r a x", a=2), in0=xin[:, :, 0:2, :], in1=xin[:, :, 2:4, :], op=ALU.add)
-                TT(out=df[:].rearrange("p r (a x) -> p r a x", a=2), in0=xin[:, :, 0:2, :], in1=xin[:, :, 2:4, :], op=ALU.subtract)
-                sm5 = sm[:].rearrange("p r (a j y) -> p r a j y", a=2, j=l)
-                df5 = df[:].rearrange("p r (a j y) -> p r a j y", a=2, j=l)
-                nxt = fft.tile([P, 2, G * Q], F32, tag=("vb", "va", "vb")[st])
-                nxt_v = nxt[:].rearrange("p r (j h y) -> p r j h y", j=l, h=4)
-                TT(out=nxt_v[:, :, :, 0, :], in0=sm5[:, :, 0, :, :], in1=sm5[:, :, 1, :, :], op=ALU.add)
+
+                def jy(ap):
+                    return ap.rearrange("p (j y) -> p j y", j=l)
+
+                def rjy(ap):
+                    return ap.rearrange("p r (j y) -> p r j y", j=l)
+
+                x = cur[:].rearrange("p r (h x) -> p r h x", h=8)
+                s = fft.tile([P, 2, 4, x8], F32, tag="s")
+                d = fft.tile([P, 2, 4, x8], F32, tag="d")
+                TT(out=s[:], in0=x[:, :, 0:4, :], in1=x[:, :, 4:8, :], op=ALU.add)
+                TT(out=d[:], in0=x[:, :, 0:4, :], in1=x[:, :, 4:8, :], op=ALU.subtract)
                 if l > 1:
-                    y3 = fft.tile([P, 2, 3 * x4], F32, tag="y3")
-                    o3 = y3[:].rearrange("p r (j h y) -> p r j h y", j=l, h=3)
-                    off = 0
+                    nxt = fft.tile([P, 2, G * Q], F32, tag="va")
+                    y7 = fft.tile([P, 2, 7 * x8], F32, tag="y7")
+                    yv = y7[:].rearrange("p r (j h y) -> p r j h y", j=l, h=7)
                 else:
-                    o3 = nxt_v
-                    off = 1
-                TT(out=o3[:, :, :, off + 1, :], in0=sm5[:, :, 0, :, :], in1=sm5[:, :, 1, :, :], op=ALU.subtract)
-                TT(out=o3[:, 0, :, off, :], in0=df5[:, 0, 0, :, :], in1=df5[:, 1, 1, :, :], op=ALU.add)
-                TT(out=o3[:, 1, :, off, :], in0=df5[:, 1, 0, :, :], in1=df5[:, 0, 1, :, :], op=ALU.subtract)
-                TT(out=o3[:, 0, :, off + 2, :], in0=df5[:, 0, 0, :, :], in1=df5[:, 1, 1, :, :], op=ALU.subtract)
-                TT(out=o3[:, 1, :, off + 2, :], in0=df5[:, 1, 0, :, :], in1=df5[:, 0, 1, :, :], op=ALU.add)
+                    nxt = vin
+                    yv = None
+                nv = nxt[:].rearrange("p r (j h y) -> p r j h y", j=l, h=8)
+
+                def dst(h):
+                    if yv is None or h == 0:
+                        return nv[:, :, :, h, :]
+                    return yv[:, :, :, h - 1, :]
+
+                ss = fft.tile([P, 2, 2, x8], F32, tag="ss")
+                sd = fft.tile([P, 2, 2, x8], F32, tag="sd")
+                TT(out=ss[:], in0=s[:, :, 0:2, :], in1=s[:, :, 2:4, :], op=ALU.add)
+                TT(out=sd[:], in0=s[:, :, 0:2, :], in1=s[:, :, 2:4, :], op=ALU.subtract)
+                TT(out=dst(0), in0=rjy(ss[:, :, 0, :]), in1=rjy(ss[:, :, 1, :]), op=ALU.add)
+                TT(out=dst(4), in0=rjy(ss[:, :, 0, :]), in1=rjy(ss[:, :, 1, :]), op=ALU.subtract)
+                TT(out=dst(2)[:, 0], in0=jy(sd[:, 0, 0, :]), in1=jy(sd[:, 1, 1, :]), op=ALU.add)
+                TT(out=dst(2)[:, 1], in0=jy(sd[:, 1, 0, :]), in1=jy(sd[:, 0, 1, :]), op=ALU.subtract)
+                TT(out=dst(6)[:, 0], in0=jy(sd[:, 0, 0, :]), in1=jy(sd[:, 1, 1, :]), op=ALU.subtract)
+                TT(out=dst(6)[:, 1], in0=jy(sd[:, 1, 0, :]), in1=jy(sd[:, 0, 1, :]), op=ALU.add)
+                pp = fft.tile([P, 2, x8], F32, tag="pp")
+                mm = fft.tile([P, 2, x8], F32, tag="mm")
+                TT(out=pp[:], in0=d[:, 0, 1:4:2, :], in1=d[:, 1, 1:4:2, :], op=ALU.add)
+                TT(out=mm[:], in0=d[:, 1, 1:4:2, :], in1=d[:, 0, 1:4:2, :], op=ALU.subtract)
+                e02p = fft.tile([P, 2, x8], F32, tag="e02p")
+                e02m = fft.tile([P, 2, x8], F32, tag="e02m")
+                e13p = fft.tile([P, 2, x8], F32, tag="e13p")
+                e13m = fft.tile([P, 2, x8], F32, tag="e13m")
+                TT(out=e02p[:, 0, :], in0=d[:, 0, 0, :], in1=d[:, 1, 2, :], op=ALU.add)
+                TT(out=e02p[:, 1, :], in0=d[:, 1, 0, :], in1=d[:, 0, 2, :], op=ALU.subtract)
+                TT(out=e13p[:, 0, :], in0=pp[:, 0, :], in1=mm[:, 1, :], op=ALU.add)
+                TT(out=e13p[:, 1, :], in0=mm[:, 0, :], in1=pp[:, 1, :], op=ALU.subtract)
+                for r in range(2):
+                    STT(out=dst(1)[:, r], in0=jy(e13p[:, r, :]), scalar=RHO, in1=jy(e02p[:, r, :]), op0=ALU.mult, op1=ALU.add)
+                    STT(out=dst(5)[:, r], in0=jy(e13p[:, r, :]), scalar=-RHO, in1=jy(e02p[:, r, :]), op0=ALU.mult, op1=ALU.add)
+                TT(out=e02m[:, 0, :], in0=d[:, 0, 0, :], in1=d[:, 1, 2, :], op=ALU.subtract)
+                TT(out=e02m[:, 1, :], in0=d[:, 1, 0, :], in1=d[:, 0, 2, :], op=ALU.add)
+                TT(out=e13m[:, 0, :], in0=pp[:, 0, :], in1=mm[:, 1, :], op=ALU.subtract)
+                TT(out=e13m[:, 1, :], in0=mm[:, 0, :], in1=pp[:, 1, :], op=ALU.add)
+                STT(out=dst(3)[:, 0], in0=jy(e13m[:, 1, :]), scalar=RHO, in1=jy(e02m[:, 0, :]), op0=ALU.mult, op1=ALU.add)
+                STT(out=dst(3)[:, 1], in0=jy(e13m[:, 0, :]), scalar=-RHO, in1=jy(e02m[:, 1, :]), op0=ALU.mult, op1=ALU.add)
+                STT(out=dst(7)[:, 0], in0=jy(e13m[:, 1, :]), scalar=-RHO, in1=jy(e02m[:, 0, :]), op0=ALU.mult, op1=ALU.add)
+                STT(out=dst(7)[:, 1], in0=jy(e13m[:, 0, :]), scalar=RHO, in1=jy(e02m[:, 1, :]), op0=ALU.mult, op1=ALU.add)
                 if l > 1:
-                    tw = tw_tab[st]
-                    shape = [P, 2, 3 * l, y]
-                    y3c = y3[:].rearrange("p r (c y) -> p r c y", c=3 * l)
-                    m1 = fft.tile([P, 2, 3 * x4], F32, tag="m1")
-                    m2 = fft.tile([P, 2, 3 * x4], F32, tag="m2")
-                    TT(out=m1[:].rearrange("p r (c y) -> p r c y", c=3 * l), in0=y3c,
-                       in1=tw[:, 0:1, :].unsqueeze(3).to_broadcast(shape), op=ALU.mult)
-                    TT(out=m2[:].rearrange("p r (c y) -> p r c y", c=3 * l), in0=y3c,
+                    shape = [P, 2, 7 * l, y]
+                    y7c = y7[:].rearrange("p r (c y) -> p r c y", c=7 * l)
+                    m2 = fft.tile([P, 2, 7 * x8], F32, tag="m2")
+                    TT(out=m2[:].rearrange("p r (c y) -> p r c y", c=7 * l), in0=y7c,
                        in1=tw.rearrange("p (a b) c -> p a b c", b=2)[:, :, 1, :].unsqueeze(3).to_broadcast(shape), op=ALU.mult)
-                    m1v = m1[:].rearrange("p r (j z) -> p r j z", j=l)
+                    TT(out=y7c, in0=y7c, in1=tw[:, 0:1, :].unsqueeze(3).to_broadcast(shape), op=ALU.mult)
+                    m1v = y7[:].rearrange("p r (j z) -> p r j z", j=l)
                     m2v = m2[:].rearrange("p r (j z) -> p r j z", j=l)
                     nz = nxt[:].rearrange("p r (j z) -> p r j z", j=l)
-                    TT(out=nz[:, 0, :, y:4 * y], in0=m1v[:, 0, :, :], in1=m2v[:, 1, :, :], op=ALU.add)
-                    TT(out=nz[:, 1, :, y:4 * y], in0=m1v[:, 1, :, :], in1=m2v[:, 0, :, :], op=ALU.add)
+                    TT(out=nz[:, 0, :, y:8 * y], in0=m1v[:, 0, :, :], in1=m2v[:, 1, :, :], op=ALU.add)
+                    TT(out=nz[:, 1, :, y:8 * y], in0=m1v[:, 1, :, :], in1=m2v[:, 0, :, :], op=ALU.add)
                 cur = nxt
-            fin = cur[:].rearrange("p r (h y) -> p r h y", h=4)
-            for hb in (0, 2, 1, 3):
-                nc.scalar.activation(out=fin[:, :, hb, :], in_=fin[:, :, hb, :], func=AF.Square)
-            started[b] = cur
+            fin = cur[:].rearrange("p r (h y) -> p r h y", h=8)
+            for first, step in GROUPS:
+                nc.scalar.activation(out=fin[:, :, first:8:step, :], in_=fin[:, :, first:8:step, :], func=AF.Square)
 
         def finish(b):
             vin, thq, sq0 = per_batch[b]
             TB = BLK * BATCHES[b][1]
-            sqv = started[b][:].rearrange("p r (g s t) -> p r g s t", s=3, t=TB)
+            sqv = vin[:].rearrange("p r (h k z) -> p r h k z", h=8, k=8)
             pw = fft.tile([P, G, 4, TB], F32, tag="pw")
+            pwv = pw[:].rearrange("p (h k) s t -> p h k (s t)", h=8)
             TT(out=pw[:, :, 0, :], in0=sq0[:, 0, :, :], in1=sq0[:, 1, :, :], op=ALU.add)
-            for hb in (0, 2, 1, 3):
-                gs = slice(16 * hb, 16 * hb + 16)
-                TT(out=pw[:, gs, 1:4, :], in0=sqv[:, 0, gs, :, :], in1=sqv[:, 1, gs, :, :], op=ALU.add)
+            for first, step in GROUPS:
+                TT(out=pwv[:, first:8:step, :, TB:4 * TB], in0=sqv[:, 0, first:8:step, :, :], in1=sqv[:, 1, first:8:step, :, :], op=ALU.add)
             thv = thq[:].rearrange("p h g t -> p g h t")
             for sig in range(2):
                 half = pw[:, :, 2 * sig:2 * sig + 2, :]

@@ -22,33 +22,42 @@ LAGS = 127
 TILES = B // P
 BLK = 4
 NBLK = TILES // BLK
-BATCHES = ((0, 1), (1, 2), (3, 2), (5, 2), (7, 1))
-NB = len(BATCHES)
-TBMAX = 8
 G = 64
-GROUPS = ((0, 2), (1, 4), (3, 4))
+FAST = ((0, 1), (1, 0), (1, 1))
+BATCHES = ((0, 1), (1, 2), (3, 2), (5, 2), (7, 1))
+SHARED = 2
+EIGHTHS = ((0, 2), (1, 4), (3, 4))
+RHO = math.sqrt(0.5)
 
 FLOPS = 2 * B * H * (H + N) + 2 * 2 * B * (N * LAGS // 2)
 
 
 def tile_qdtssolveronnx_pa_kernel(tc, h1, w_hid2, b_hid2, w_out, b_out, norm_root, T, out_0, out_1, out_2, out_3):
     nc = tc.nc
+    tensor_tensor = nc.vector.tensor_tensor
+    mul_add = nc.vector.scalar_tensor_tensor
     with ExitStack() as ctx:
         keep = ctx.enter_context(tc.tile_pool(name="keep", bufs=1))
-        h1p = ctx.enter_context(tc.tile_pool(name="h1p", bufs=3))
+        h1_pool = ctx.enter_context(tc.tile_pool(name="h1_pool", bufs=3))
         stage = ctx.enter_context(tc.tile_pool(name="stage", bufs=2))
-        batch = ctx.enter_context(tc.tile_pool(name="batch", bufs=2))
+        z_pool = ctx.enter_context(tc.tile_pool(name="z_pool", bufs=3))
+        batch_pool = ctx.enter_context(tc.tile_pool(name="batch_pool", bufs=2))
         fft = ctx.enter_context(tc.tile_pool(name="fft", bufs=1))
-        zpool = ctx.enter_context(tc.tile_pool(name="zpool", bufs=3))
-        ps_tp = ctx.enter_context(tc.psum_pool(name="ps_tp", bufs=1))
-        ps_m1 = ctx.enter_context(tc.psum_pool(name="ps_m1", bufs=2))
-        ps_m2 = ctx.enter_context(tc.psum_pool(name="ps_m2", bufs=1))
-        psum = ctx.enter_context(tc.psum_pool(name="psum", bufs=4))
+        ps_in = ctx.enter_context(tc.psum_pool(name="ps_in", bufs=1))
+        ps_h2 = ctx.enter_context(tc.psum_pool(name="ps_h2", bufs=2))
+        ps_x = ctx.enter_context(tc.psum_pool(name="ps_x", bufs=1))
+        ps_spec = ctx.enter_context(tc.psum_pool(name="ps_spec", bufs=4))
 
         w1_sb = keep.tile([P, 4, H], BF16)
         nc.sync.dma_start(out=w1_sb[:], in_=w_hid2.rearrange("(p c) k -> p c k", c=4))
-        h1_v = h1.rearrange("(p t) k -> p t k", t=TILES)
-        w2_sb = keep.tile([P, H], BF16)
+        h1_rows = h1.rearrange("(p t) k -> p t k", t=TILES)
+        h1_tiles = {}
+
+        def load_h1(i):
+            h1_sb = h1_pool.tile([P, BLK, H], BF16, name="h1_sb")
+            nc.sync.dma_start(out=h1_sb[:], in_=h1_rows[:, BLK * i:BLK * (i + 1), :])
+            h1_tiles[i] = h1_sb
+
         b1_bf = keep.tile([P, 4], BF16)
         b2_bf = keep.tile([P, 1], BF16)
         nr_bf = keep.tile([P, TILES], BF16)
@@ -58,53 +67,63 @@ def tile_qdtssolveronnx_pa_kernel(tc, h1, w_hid2, b_hid2, w_out, b_out, norm_roo
             nc.scalar.dma_start(out=nr_bf[:], in_=norm_root.rearrange("(p t) o -> p (t o)", t=TILES))
         t_pad = keep.tile([P, TILES, N], BF16)
         nc.vector.memset(t_pad[:], 0.0)
+        ident = keep.tile([P, P], F32)
+        make_identity(nc, ident[:])
+        ident_bf = keep.tile([P, P], BF16)
+        make_identity(nc, ident_bf[:])
+        load_h1(0)
+        w2_sb = keep.tile([P, H], BF16)
+        nc.sync.dma_start(out=w2_sb[:], in_=w_out)
+        load_h1(1)
+        nc.sync.dma_start(out=t_pad[:, :, 0:LAGS], in_=T.rearrange("(p t) c -> p t c", t=TILES))
 
         def sines(phase, width, name):
             nc.vector.tensor_single_scalar(out=phase, in_=phase, scalar=511, op=ALU.bitwise_and)
-            ang = fft.tile([P, width], F32, name=name + "_ang", tag="y7")
-            nc.vector.tensor_scalar(out=ang[:], in0=phase, scalar1=-256.0, scalar2=None, op0=ALU.add)
-            edge = fft.tile([P, width], F32, name=name + "_edge", tag="m2")
-            nc.vector.tensor_scalar(out=edge[:], in0=ang[:], scalar1=-256.0, scalar2=256.0, op0=ALU.is_equal, op1=ALU.mult)
-            nc.vector.tensor_tensor(out=ang[:], in0=ang[:], in1=edge[:], op=ALU.add)
-            tab = keep.tile([P, width], F32, name=name + "_tab")
-            nc.scalar.activation(out=tab[:], in_=ang[:], func=AF.Sin, scale=math.pi / 256.0)
-            return tab
+            angle = fft.tile([P, width], F32, name=name + "_angle", tag="mid")
+            nc.vector.tensor_scalar(out=angle[:], in0=phase, scalar1=-256.0, scalar2=None, op0=ALU.add)
+            edge = fft.tile([P, width], F32, name=name + "_edge", tag="cross")
+            nc.vector.tensor_scalar(out=edge[:], in0=angle[:], scalar1=-256.0, scalar2=256.0, op0=ALU.is_equal, op1=ALU.mult)
+            nc.vector.tensor_tensor(out=angle[:], in0=angle[:], in1=edge[:], op=ALU.add)
+            table = keep.tile([P, width], F32, name=name + "_table")
+            nc.scalar.activation(out=table[:], in_=angle[:], func=AF.Sin, scale=math.pi / 256.0)
+            return table
+
+        COS = 256 + 128
 
         W_TW = 4 * 56
-        W_ALL = W_TW + N
-        ph = keep.tile([P, W_ALL], I32)
-        tw_ph = ph[:, 0:W_TW].rearrange("p (k j h) -> p k j h", k=4, h=7)
-        for hh in range(1, 8):
-            nc.gpsimd.iota(tw_ph[:, :, :, hh - 1], pattern=[[128, 4], [8 * hh, 8]], base=384, channel_multiplier=0)
-        nc.gpsimd.iota(ph[:, W_ALL - N:W_ALL], pattern=[[-509, N]], base=LAGS * 509 + 384, channel_multiplier=0)
-        tabs = sines(ph[:], W_ALL, "row")
+        row_phase = keep.tile([P, W_TW + N], I32)
+        tw_phase = row_phase[:, 0:W_TW].rearrange("p (k j h) -> p k j h", k=4, h=7)
+        for h in range(1, 8):
+            nc.gpsimd.iota(tw_phase[:, :, :, h - 1], pattern=[[128, 4], [8 * h, 8]], base=COS, channel_multiplier=0)
+        LAST_FREQ = 4 * (N - 1) + 1
+        nc.gpsimd.iota(row_phase[:, W_TW:W_TW + N], pattern=[[-LAST_FREQ, N]], base=LAGS * LAST_FREQ + COS, channel_multiplier=0)
+        row_table = sines(row_phase[:], W_TW + N, "row")
+        twiddle = row_table[:, 0:W_TW].rearrange("p (k j h) -> p k j h", k=4, h=7)
         last_col = keep.tile([P, N], F32)
-        nc.vector.tensor_scalar(out=last_col[:], in0=tabs[:, W_ALL - N:W_ALL], scalar1=2.0, scalar2=None, op0=ALU.mult)
-        tw = tabs[:, 0:W_TW].rearrange("p (k c) -> p k c", k=4)
+        nc.vector.tensor_scalar(out=last_col[:], in0=row_table[:, W_TW:W_TW + N], scalar1=2.0, scalar2=None, op0=ALU.mult)
 
-        pidx = keep.tile([P, 2], I32)
-        nc.gpsimd.iota(pidx[:, 0:1], pattern=[[0, 1]], base=0, channel_multiplier=1)
-        nc.gpsimd.iota(pidx[:, 1:2], pattern=[[0, 1]], base=LAGS, channel_multiplier=-1)
-        pf = keep.tile([P, 2], F32)
-        nc.vector.tensor_copy(out=pf[:], in_=pidx[:])
+        p_index = keep.tile([P, 2], I32)
+        nc.gpsimd.iota(p_index[:, 0:1], pattern=[[0, 1]], base=0, channel_multiplier=1)
+        nc.gpsimd.iota(p_index[:, 1:2], pattern=[[0, 1]], base=LAGS, channel_multiplier=-1)
+        p_float = keep.tile([P, 2], F32)
+        nc.vector.tensor_copy(out=p_float[:], in_=p_index[:])
         freq = keep.tile([P, 2, G], I32)
         nc.gpsimd.iota(freq[:], pattern=[[4, 2], [8, G]], base=1, channel_multiplier=0)
-        mph = keep.tile([P, 4 * G + 4], I32)
+        mat_phase = keep.tile([P, 4 * G + 4], I32)
         for hf in range(2):
-            nc.gpsimd.iota(mph[:, 4 * G + 2 * hf:4 * G + 2 * hf + 2], pattern=[[128, 2]], base=384, channel_multiplier=1 + 4 * hf)
-        nc.vector.tensor_scalar(out=mph[:, 0:G], in0=freq[:, 0, :], scalar1=pf[:, 0:1], scalar2=384.0, op0=ALU.mult, op1=ALU.add)
-        nc.vector.tensor_scalar(out=mph[:, G:2 * G], in0=freq[:, 0, :], scalar1=pf[:, 0:1], scalar2=256.0, op0=ALU.mult, op1=ALU.add)
-        nc.vector.tensor_scalar(out=mph[:, 2 * G:4 * G], in0=freq[:].rearrange("p h g -> p (h g)"), scalar1=pf[:, 1:2], scalar2=384.0, op0=ALU.mult, op1=ALU.add)
-        mats = sines(mph[:], 4 * G + 4, "mat")
-        cvec = mats[:, 4 * G:4 * G + 4]
-        fx = mats[:, 0:2 * G]
-        ct = keep.tile([P, 2 * G], F32)
-        nc.vector.tensor_scalar(out=ct[:], in0=mats[:, 2 * G:4 * G], scalar1=2.0, scalar2=None, op0=ALU.mult)
+            nc.gpsimd.iota(mat_phase[:, 4 * G + 2 * hf:4 * G + 2 * hf + 2], pattern=[[128, 2]], base=COS, channel_multiplier=1 + 4 * hf)
+        nc.vector.tensor_scalar(out=mat_phase[:, 0:G], in0=freq[:, 0, :], scalar1=p_float[:, 0:1], scalar2=float(COS),
+                                op0=ALU.mult, op1=ALU.add)
+        nc.vector.tensor_scalar(out=mat_phase[:, G:2 * G], in0=freq[:, 0, :], scalar1=p_float[:, 0:1], scalar2=256.0,
+                                op0=ALU.mult, op1=ALU.add)
+        nc.vector.tensor_scalar(out=mat_phase[:, 2 * G:4 * G], in0=freq[:].rearrange("p h g -> p (h g)"), scalar1=p_float[:, 1:2],
+                                scalar2=float(COS), op0=ALU.mult, op1=ALU.add)
+        mat_table = sines(mat_phase[:], 4 * G + 4, "mat")
+        x_matrix = mat_table[:, 0:2 * G]
+        t_matrix = keep.tile([P, 2 * G], F32)
+        nc.vector.tensor_scalar(out=t_matrix[:], in0=mat_table[:, 2 * G:4 * G], scalar1=2.0, scalar2=None, op0=ALU.mult)
+        twist = mat_table[:, 4 * G:4 * G + 4]
 
-        ident = keep.tile([P, P], F32)
-        make_identity(nc, ident[:])
-        identb = keep.tile([P, P], BF16)
-        make_identity(nc, identb[:])
         b1 = keep.tile([P, 4], F32)
         nc.vector.tensor_copy(out=b1[:], in_=b1_bf[:])
         b2 = keep.tile([P, 1], F32)
@@ -112,175 +131,159 @@ def tile_qdtssolveronnx_pa_kernel(tc, h1, w_hid2, b_hid2, w_out, b_out, norm_roo
         nr = keep.tile([P, TILES], F32)
         nc.vector.tensor_copy(out=nr[:], in_=nr_bf[:])
 
-        h1_tiles = {}
-
-        def load_h1(i):
-            h1_sb = h1p.tile([P, BLK, H], BF16, name="h1_sb")
-            nc.sync.dma_start(out=h1_sb[:], in_=h1_v[:, BLK * i:BLK * (i + 1), :])
-            h1_tiles[i] = h1_sb
-
-        load_h1(0)
-        nc.sync.dma_start(out=w2_sb[:], in_=w_out)
-        load_h1(1)
-        nc.sync.dma_start(out=t_pad[:, :, 0:LAGS], in_=T.rearrange("(p t) c -> p t c", t=TILES))
-
-        w1g = keep.tile([P, 4 * P, 4], BF16, align_bytes=64)
-        w1g32 = w1g[:].bitcast(F32)
-        w1_32 = w1_sb[:].bitcast(F32)
+        w1_grouped = keep.tile([P, 4 * P, 4], BF16, align_bytes=64)
+        w1_grouped32 = w1_grouped[:].bitcast(F32)
+        w1_words = w1_sb[:].bitcast(F32)
         for a in range(2):
-            pw = ps_tp.tile([P, 2, 2, P], F32, tag="tp")
+            w1_t = ps_in.tile([P, 2, 2, P], F32, tag="in")
             for u in range(2):
-                for cc in range(2):
-                    nc.tensor.transpose(pw[:, u, cc, :], w1_32[:, 2 * a + cc, P * u:P * (u + 1)], ident[:])
-            nc.vector.tensor_copy(out=w1g32[:, 2 * P * a:2 * P * (a + 1), :], in_=pw[:].rearrange("q u c m -> q (c m) u"))
-        w1c = keep.tile([P, 4 * P], U32, align_bytes=64)
-        w1s = keep.tile([P, 4 * P], U8, align_bytes=64)
-        nc.vector.quantize_mx(out=w1c[:].bitcast(FP8X4), scales=w1s[:], in_=w1g[:].rearrange("q n f -> q (n f)"))
-
-        w2g = keep.tile([P, P, 4], BF16, align_bytes=64)
-        w2_32 = w2_sb[:].bitcast(F32).rearrange("p (m u) -> p u m", u=2)
-        pw2 = ps_tp.tile([P, 2, P], F32, tag="tp")
+                for c in range(2):
+                    nc.tensor.transpose(w1_t[:, u, c, :], w1_words[:, 2 * a + c, P * u:P * (u + 1)], ident[:])
+            nc.vector.tensor_copy(out=w1_grouped32[:, 2 * P * a:2 * P * (a + 1), :], in_=w1_t[:].rearrange("q u c m -> q (c m) u"))
+        w1_codes = keep.tile([P, 4 * P], U32, align_bytes=64)
+        w1_scales = keep.tile([P, 4 * P], U8, align_bytes=64)
+        nc.vector.quantize_mx(out=w1_codes[:].bitcast(FP8X4), scales=w1_scales[:], in_=w1_grouped[:].rearrange("q n f -> q (n f)"))
+        w2_grouped = keep.tile([P, P, 4], BF16, align_bytes=64)
+        w2_words = w2_sb[:].bitcast(F32).rearrange("p (m u) -> p u m", u=2)
+        w2_t = ps_in.tile([P, 2, P], F32, tag="in")
         for u in range(2):
-            nc.tensor.transpose(pw2[:, u, :], w2_32[:, u, :], ident[:])
-        nc.vector.tensor_copy(out=w2g[:].bitcast(F32), in_=pw2[:].rearrange("q u n -> q n u"))
-        w2c = keep.tile([P, P], U32, align_bytes=64)
-        w2s = keep.tile([P, P], U8, align_bytes=64)
-        nc.vector.quantize_mx(out=w2c[:].bitcast(FP8X4), scales=w2s[:], in_=w2g[:].rearrange("q n f -> q (n f)"))
+            nc.tensor.transpose(w2_t[:, u, :], w2_words[:, u, :], ident[:])
+        nc.vector.tensor_copy(out=w2_grouped[:].bitcast(F32), in_=w2_t[:].rearrange("q u n -> q n u"))
+        w2_codes = keep.tile([P, P], U32, align_bytes=64)
+        w2_scales = keep.tile([P, P], U8, align_bytes=64)
+        nc.vector.quantize_mx(out=w2_codes[:].bitcast(FP8X4), scales=w2_scales[:], in_=w2_grouped[:].rearrange("q n f -> q (n f)"))
 
-        o0 = out_0.rearrange("(p t) j -> p t j", t=TILES)
-        o2 = out_2.rearrange("(p t) j -> p t j", t=TILES)
-        r0 = keep.tile([P, 2, TILES], F32)
-        acc_d = keep.tile([P, 2, NB], F32)
+        x_rows = keep.tile([P, 2, TILES, N], F32)
+        x_out = (out_0.rearrange("(p t) j -> p t j", t=TILES), out_2.rearrange("(p t) j -> p t j", t=TILES))
+        d2_sums = keep.tile([P, 2, len(BATCHES)], F32)
         per_batch = {}
+        x_cols = {}
 
-        def front(i):
-            b = [k for k, (first, cnt) in enumerate(BATCHES) if first <= i < first + cnt][0]
-            tb = BLK * BATCHES[b][1]
-            sub = slice(BLK * (i - BATCHES[b][0]), BLK * (i - BATCHES[b][0]) + BLK)
-            if b not in per_batch:
-                xq_new = batch.tile([P, 2, G * 3 * tb], F32, name="vin")
-                thq_new = batch.tile([P, 2, G, tb], F32, name="thq")
-                sq_new = batch.tile([P, 2, G, tb], F32, name="sq0")
-                per_batch[b] = (xq_new, thq_new, sq_new)
-            early = i <= 2
-            vin, thq, sq0 = per_batch[b]
-            vin_v = vin[:].rearrange("p r (n s t) -> p r n s t", s=3, t=tb)
+        def place(i):
+            b = [k for k, (first, count) in enumerate(BATCHES) if first <= i < first + count][0]
+            at = BLK * (i - BATCHES[b][0])
+            return b, BLK * BATCHES[b][1], slice(at, at + BLK)
+
+        def network(i):
+            shared = i < SHARED
             if i + 2 < NBLK:
                 load_h1(i + 2)
-            h1_32 = h1_tiles[i][:].bitcast(F32)
-            h1g = stage.tile([P, BLK * P, 4], BF16, align_bytes=64)
-            h1g32 = h1g[:].bitcast(F32)
+            h1_words = h1_tiles[i][:].bitcast(F32)
+            h1_grouped = stage.tile([P, BLK * P, 4], BF16, align_bytes=64)
+            h1_grouped32 = h1_grouped[:].bitcast(F32)
             for a in range(2):
-                pt = ps_tp.tile([P, 2, 2, P], F32, tag="tp")
+                h1_t = ps_in.tile([P, 2, 2, P], F32, tag="in")
                 for u in range(2):
-                    for tt in range(2):
-                        nc.tensor.transpose(pt[:, u, tt, :], h1_32[:, 2 * a + tt, P * u:P * (u + 1)], ident[:])
-                if early:
-                    nc.vector.tensor_copy(out=h1g32[:, 2 * P * a:2 * P * (a + 1), :], in_=pt[:].rearrange("q u t p -> q (t p) u"))
+                    for t in range(2):
+                        nc.tensor.transpose(h1_t[:, u, t, :], h1_words[:, 2 * a + t, P * u:P * (u + 1)], ident[:])
+                if shared:
+                    nc.vector.tensor_copy(out=h1_grouped32[:, 2 * P * a:2 * P * (a + 1), :], in_=h1_t[:].rearrange("q u t p -> q (t p) u"))
                 else:
-                    nc.scalar.copy(out=h1g32[:, 2 * P * a:2 * P * (a + 1), :], in_=pt[:].rearrange("q u t p -> q (t p) u"))
-            h1c = stage.tile([P, BLK * P], U32, align_bytes=64)
-            h1s = stage.tile([P, BLK * P], U8, align_bytes=64)
-            nc.vector.quantize_mx(out=h1c[:].bitcast(FP8X4), scales=h1s[:], in_=h1g[:].rearrange("q n f -> q (n f)"))
+                    nc.scalar.copy(out=h1_grouped32[:, 2 * P * a:2 * P * (a + 1), :], in_=h1_t[:].rearrange("q u t p -> q (t p) u"))
+            h1_codes = stage.tile([P, BLK * P], U32, align_bytes=64)
+            h1_scales = stage.tile([P, BLK * P], U8, align_bytes=64)
+            nc.vector.quantize_mx(out=h1_codes[:].bitcast(FP8X4), scales=h1_scales[:], in_=h1_grouped[:].rearrange("q n f -> q (n f)"))
 
-            h2p = stage.tile([P, 4, BLK * P], BF16)
+            h2_planes = stage.tile([P, 4, BLK * P], BF16)
             for c in range(4):
-                p1 = ps_m1.tile([P, BLK * P], F32, tag="m1")
-                nc.tensor.matmul_mx(out=p1[:], lhsT=w1c[:, P * c:P * (c + 1)].bitcast(FP8X4), lhsT_scale=w1s[:, P * c:P * (c + 1)],
-                                    rhs=h1c[:].bitcast(FP8X4), rhs_scale=h1s[:], start=True, stop=True)
-                if early and c % 2 == 1:
-                    nc.vector.tensor_scalar(out=h2p[:, c, :], in0=p1[:], scalar1=b1[:, c:c + 1], scalar2=0.0, op0=ALU.add, op1=ALU.max)
+                h2_acc = ps_h2.tile([P, BLK * P], F32, tag="h2")
+                nc.tensor.matmul_mx(out=h2_acc[:], lhsT=w1_codes[:, P * c:P * (c + 1)].bitcast(FP8X4),
+                                    lhsT_scale=w1_scales[:, P * c:P * (c + 1)],
+                                    rhs=h1_codes[:].bitcast(FP8X4), rhs_scale=h1_scales[:], start=True, stop=True)
+                if shared and c % 2 == 1:
+                    nc.vector.tensor_scalar(out=h2_planes[:, c, :], in0=h2_acc[:], scalar1=b1[:, c:c + 1], scalar2=0.0,
+                                            op0=ALU.add, op1=ALU.max)
                 else:
-                    nc.scalar.activation(out=h2p[:, c, :], in_=p1[:], func=AF.Relu, bias=b1[:, c:c + 1], scale=1.0)
-            h2g = stage.tile([P, BLK * P, 4], BF16, align_bytes=64)
-            h2g_runs = h2g[:].rearrange("m (a i) c -> m a c i", i=4)
-            h2p_runs = h2p[:].rearrange("m c (a i) -> m a c i", i=4)
-            if early:
-                nc.vector.tensor_copy(out=h2g_runs, in_=h2p_runs)
+                    nc.scalar.activation(out=h2_planes[:, c, :], in_=h2_acc[:], func=AF.Relu, bias=b1[:, c:c + 1], scale=1.0)
+            h2_grouped = stage.tile([P, BLK * P, 4], BF16, align_bytes=64)
+            grouped_runs = h2_grouped[:].rearrange("m (a i) c -> m a c i", i=4)
+            plane_runs = h2_planes[:].rearrange("m c (a i) -> m a c i", i=4)
+            if shared:
+                nc.vector.tensor_copy(out=grouped_runs, in_=plane_runs)
             else:
-                nc.scalar.copy(out=h2g_runs, in_=h2p_runs)
-            h2c = stage.tile([P, BLK * P], U32, align_bytes=64)
-            h2s = stage.tile([P, BLK * P], U8, align_bytes=64)
-            nc.vector.quantize_mx(out=h2c[:].bitcast(FP8X4), scales=h2s[:], in_=h2g[:].rearrange("m n f -> m (n f)"))
+                nc.scalar.copy(out=grouped_runs, in_=plane_runs)
+            h2_codes = stage.tile([P, BLK * P], U32, align_bytes=64)
+            h2_scales = stage.tile([P, BLK * P], U8, align_bytes=64)
+            nc.vector.quantize_mx(out=h2_codes[:].bitcast(FP8X4), scales=h2_scales[:], in_=h2_grouped[:].rearrange("m n f -> m (n f)"))
 
-            p2 = ps_m2.tile([P, BLK * P], F32, tag="m2")
-            nc.tensor.matmul_mx(out=p2[:], lhsT=w2c[:].bitcast(FP8X4), lhsT_scale=w2s[:],
-                                rhs=h2c[:].bitcast(FP8X4), rhs_scale=h2s[:], start=True, stop=True)
-            yt = stage.tile([P, BLK * P], F32)
-            nc.scalar.activation(out=yt[:], in_=p2[:], func=AF.Identity, bias=b2[:, 0:1], scale=1.0)
-            py = ps_m2.tile([P, BLK, P], F32, tag="m2")
+            y_acc = ps_x.tile([P, BLK * P], F32, tag="x")
+            nc.tensor.matmul_mx(out=y_acc[:], lhsT=w2_codes[:].bitcast(FP8X4), lhsT_scale=w2_scales[:],
+                                rhs=h2_codes[:].bitcast(FP8X4), rhs_scale=h2_scales[:], start=True, stop=True)
+            y_cols = stage.tile([P, BLK * P], F32)
+            nc.scalar.activation(out=y_cols[:], in_=y_acc[:], func=AF.Identity, bias=b2[:, 0:1], scale=1.0)
+            y_rows = ps_x.tile([P, BLK, P], F32, tag="x")
             for t in range(BLK):
-                nc.tensor.transpose(py[:, t, :], yt[:, P * t:P * (t + 1)], ident[:])
-            xr = stage.tile([P, BLK, N], F32)
-            xc = stage.tile([P, BLK, N], F32)
+                nc.tensor.transpose(y_rows[:, t, :], y_cols[:, P * t:P * (t + 1)], ident[:])
+            tiles = slice(BLK * i, BLK * (i + 1))
             for t in range(BLK):
-                g = BLK * i + t
-                nc.scalar.activation(out=xr[:, t, :], in_=py[:, t, :], func=AF.Copy, scale=nr[:, g:g + 1])
-            nc.vector.tensor_scalar(out=xc[:], in0=xr[:], scalar1=-2.0, scalar2=2.0, op0=ALU.max, op1=ALU.min)
-            blk = slice(BLK * i, BLK * (i + 1))
-            nc.sync.dma_start(out=o0[:, blk, :], in_=xr[:])
-            nc.sync.dma_start(out=o2[:, blk, :], in_=xc[:])
+                nc.scalar.activation(out=x_rows[:, 0, BLK * i + t, :], in_=y_rows[:, t, :], func=AF.Copy,
+                                     scale=nr[:, BLK * i + t:BLK * i + t + 1])
+            nc.vector.tensor_scalar(out=x_rows[:, 1, tiles, :], in0=x_rows[:, 0, tiles, :], scalar1=-2.0, scalar2=2.0,
+                                    op0=ALU.max, op1=ALU.min)
+            for sig in range(2):
+                nc.sync.dma_start(out=x_out[sig][:, tiles, :], in_=x_rows[:, sig, tiles, :])
 
-            pxt = psum.tile([P, BLK, P], F32, tag="ps")
-            for t in range(BLK):
-                nc.tensor.transpose(pxt[:, t, :], xr[:, t, :], ident[:])
-            xt = stage.tile([P, BLK, P], F32)
-            nc.scalar.copy(out=xt[:], in_=pxt[:])
-            pxc = psum.tile([P, BLK, P], F32, tag="ps")
-            for t in range(BLK):
-                nc.tensor.transpose(pxc[:, t, :], xc[:, t, :], ident[:])
-            for s3, (src, hf) in enumerate(((pxt, 1), (pxc, 0), (pxc, 1))):
+        def inputs(i):
+            b, tb, sub = place(i)
+            if b not in per_batch:
+                v_new = batch_pool.tile([P, 2, G * 3 * tb], F32, name="v")
+                th_new = batch_pool.tile([P, 2, G, tb], F32, name="th")
+                sq0_new = batch_pool.tile([P, 2, G, tb], F32, name="sq0")
+                per_batch[b] = (v_new, th_new, sq0_new)
+            v_view = per_batch[b][0][:].rearrange("p r (n s t) -> p r n s t", s=3, t=tb)
+            cols = []
+            for sig in range(2):
+                sig_cols = ps_spec.tile([P, BLK, P], F32, tag="spec", name="sig_cols")
+                for t in range(BLK):
+                    nc.tensor.transpose(sig_cols[:, t, :], x_rows[:, sig, BLK * i + t, :], ident[:])
+                cols.append(sig_cols)
+            for s, (sig, hf) in enumerate(FAST):
                 for r in range(2):
-                    zt = zpool.tile([P, BLK, P], F32, name="zt")
-                    nc.scalar.activation(out=zt[:], in_=src[:], func=AF.Copy, scale=cvec[:, 2 * hf + r:2 * hf + r + 1])
-                    pv = psum.tile([P, BLK, P], F32, tag="ps")
+                    z_cols = z_pool.tile([P, BLK, P], F32, name="z_cols")
+                    nc.scalar.activation(out=z_cols[:], in_=cols[sig][:], func=AF.Copy, scale=twist[:, 2 * hf + r:2 * hf + r + 1])
+                    z_rows = ps_spec.tile([P, BLK, P], F32, tag="spec", name="z_rows")
                     for t in range(BLK):
-                        nc.tensor.transpose(pv[:, t, :], zt[:, t, :], ident[:])
-                    up = zpool.tile([P, G, BLK], F32, name="up")
-                    nc.scalar.copy(out=up[:], in_=pv[:, :, G:N].rearrange("p t n -> p n t"))
-                    nc.vector.tensor_tensor(out=vin_v[:, r, :, s3, sub], in0=pv[:, :, 0:G].rearrange("p t n -> p n t"), in1=up[:], op=ALU.add)
-            pf0 = psum.tile([P, BLK, P], F32, tag="ps")
+                        nc.tensor.transpose(z_rows[:, t, :], z_cols[:, t, :], ident[:])
+                    z_high = z_pool.tile([P, G, BLK], F32, name="z_high")
+                    nc.scalar.copy(out=z_high[:], in_=z_rows[:, :, G:N].rearrange("p t n -> p n t"))
+                    tensor_tensor(out=v_view[:, r, :, s, sub], in0=z_rows[:, :, 0:G].rearrange("p t n -> p n t"), in1=z_high[:], op=ALU.add)
+                if s == 0:
+                    x_cols[i] = stage.tile([P, BLK, P], F32, name="x_cols")
+                    nc.scalar.copy(out=x_cols[i][:], in_=cols[0][:])
+
+        def matrices(i):
+            b, tb, sub = place(i)
+            v, th, sq0 = per_batch[b]
+            spec0 = ps_spec.tile([P, BLK, P], F32, tag="spec")
             for t in range(BLK):
-                nc.tensor.matmul(out=pf0[:, t, :], lhsT=xt[:, t, :], rhs=fx, start=True, stop=True)
-            nc.scalar.activation(out=sq0[:, :, :, sub].rearrange("p r g t -> p (r g) t"), in_=pf0[:].rearrange("p t c -> p c t"),
+                nc.tensor.matmul(out=spec0[:, t, :], lhsT=x_cols[i][:, t, :], rhs=x_matrix, start=True, stop=True)
+            nc.scalar.activation(out=sq0[:, :, :, sub].rearrange("p r g t -> p (r g) t"), in_=spec0[:].rearrange("p t c -> p c t"),
                                  func=AF.Square)
-            ptt = psum.tile([P, BLK, P], BF16, tag="ps")
+            t_t = ps_spec.tile([P, BLK, P], BF16, tag="spec")
             for t in range(BLK):
-                nc.tensor.transpose(ptt[:, t, :], t_pad[:, BLK * i + t, :], identb[:])
-            ttr = stage.tile([P, BLK, P], F32)
-            nc.scalar.copy(out=ttr[:], in_=ptt[:])
-            pth = psum.tile([P, BLK, P], F32, tag="ps")
+                nc.tensor.transpose(t_t[:, t, :], t_pad[:, BLK * i + t, :], ident_bf[:])
+            t_cols = stage.tile([P, BLK, P], F32)
+            nc.scalar.copy(out=t_cols[:], in_=t_t[:])
+            th_acc = ps_spec.tile([P, BLK, P], F32, tag="spec")
             for t in range(BLK):
                 if BLK * i + t == TILES - 1:
-                    nc.tensor.transpose(pth[:, t, :], ttr[:, t, :], ident[:])
-                    nc.tensor.matmul(out=pth[:, t, 0:P - 1], lhsT=ttr[:, t, :], rhs=ct[:, 0:P - 1], start=True, stop=True)
+                    nc.tensor.transpose(th_acc[:, t, :], t_cols[:, t, :], ident[:])
+                    nc.tensor.matmul(out=th_acc[:, t, 0:P - 1], lhsT=t_cols[:, t, :], rhs=t_matrix[:, 0:P - 1], start=True, stop=True)
                 else:
-                    nc.tensor.matmul(out=pth[:, t, :], lhsT=ttr[:, t, :], rhs=ct[:], start=True, stop=True)
-            nc.scalar.copy(out=thq[:, :, :, sub].rearrange("p h g t -> p (h g) t"), in_=pth[:].rearrange("p t c -> p c t"))
+                    nc.tensor.matmul(out=th_acc[:, t, :], lhsT=t_cols[:, t, :], rhs=t_matrix[:], start=True, stop=True)
+            nc.scalar.copy(out=th[:, :, :, sub].rearrange("p h g t -> p (h g) t"), in_=th_acc[:].rearrange("p t c -> p c t"))
             if i == NBLK - 1:
-                fix = stage.tile([P, N], F32)
-                nc.vector.tensor_tensor(out=fix[:], in0=t_pad[:, TILES - 1, :], in1=last_col[:], op=ALU.mult)
-                nc.vector.tensor_reduce(out=thq[:, 1, G - 1, tb - 1:tb], in_=fix[:], axis=AX.X, op=ALU.add)
+                products = stage.tile([P, N], F32)
+                tensor_tensor(out=products[:], in0=t_pad[:, TILES - 1, :], in1=last_col[:], op=ALU.mult)
+                nc.vector.tensor_reduce(out=th[:, 1, G - 1, tb - 1:tb], in_=products[:], axis=AX.X, op=ALU.add)
 
-            junk = stage.tile([P, N], F32)
-            for t in range(BLK):
-                g = BLK * i + t
-                nc.scalar.activation(out=junk[:], in_=xr[:, t, :], func=AF.Square, accum_out=r0[:, 0, g:g + 1])
-                nc.scalar.activation(out=junk[:], in_=xc[:, t, :], func=AF.Square, accum_out=r0[:, 1, g:g + 1])
-
-        TT = nc.vector.tensor_tensor
-
-        STT = nc.vector.scalar_tensor_tensor
-        RHO = math.sqrt(0.5)
-
-        def stages(b):
-            TB = BLK * BATCHES[b][1]
-            Q = 3 * TB
-            x8 = 8 * Q
-            vin = per_batch[b][0]
-            cur = vin
+        def transforms(b):
+            q = 3 * BLK * BATCHES[b][1]
+            x8 = 8 * q
+            v = per_batch[b][0]
+            src = v
             for l, m in ((8, 1), (1, 8)):
-                y = m * Q
+                y = m * q
 
                 def jy(ap):
                     return ap.rearrange("p (j y) -> p j y", j=l)
@@ -288,115 +291,119 @@ def tile_qdtssolveronnx_pa_kernel(tc, h1, w_hid2, b_hid2, w_out, b_out, norm_roo
                 def rjy(ap):
                     return ap.rearrange("p r (j y) -> p r j y", j=l)
 
-                x = cur[:].rearrange("p r (h x) -> p r h x", h=8)
+                x = src[:].rearrange("p r (h x) -> p r h x", h=8)
                 s = fft.tile([P, 2, 4, x8], F32, tag="s")
                 d = fft.tile([P, 2, 4, x8], F32, tag="d")
-                TT(out=s[:], in0=x[:, :, 0:4, :], in1=x[:, :, 4:8, :], op=ALU.add)
-                TT(out=d[:], in0=x[:, :, 0:4, :], in1=x[:, :, 4:8, :], op=ALU.subtract)
-                if l > 1:
-                    nxt = fft.tile([P, 2, G * Q], F32, tag="va")
-                    y7 = fft.tile([P, 2, 7 * x8], F32, tag="y7")
-                    yv = y7[:].rearrange("p r (j h y) -> p r j h y", j=l, h=7)
-                else:
-                    nxt = vin
-                    yv = None
-                nv = nxt[:].rearrange("p r (j h y) -> p r j h y", j=l, h=8)
-
-                def dst(h):
-                    if yv is None or h == 0:
-                        return nv[:, :, :, h, :]
-                    return yv[:, :, :, h - 1, :]
-
+                tensor_tensor(out=s[:], in0=x[:, :, 0:4, :], in1=x[:, :, 4:8, :], op=ALU.add)
+                tensor_tensor(out=d[:], in0=x[:, :, 0:4, :], in1=x[:, :, 4:8, :], op=ALU.subtract)
+                dst_tile = fft.tile([P, 2, G * q], F32, tag="mid", name="mid") if l > 1 else v
+                dst = dst_tile[:].rearrange("p r (j h y) -> p r j h y", j=l, h=8)
                 ss = fft.tile([P, 2, 2, x8], F32, tag="ss")
                 sd = fft.tile([P, 2, 2, x8], F32, tag="sd")
-                TT(out=ss[:], in0=s[:, :, 0:2, :], in1=s[:, :, 2:4, :], op=ALU.add)
-                TT(out=sd[:], in0=s[:, :, 0:2, :], in1=s[:, :, 2:4, :], op=ALU.subtract)
-                TT(out=dst(0), in0=rjy(ss[:, :, 0, :]), in1=rjy(ss[:, :, 1, :]), op=ALU.add)
-                TT(out=dst(4), in0=rjy(ss[:, :, 0, :]), in1=rjy(ss[:, :, 1, :]), op=ALU.subtract)
-                TT(out=dst(2)[:, 0], in0=jy(sd[:, 0, 0, :]), in1=jy(sd[:, 1, 1, :]), op=ALU.add)
-                TT(out=dst(2)[:, 1], in0=jy(sd[:, 1, 0, :]), in1=jy(sd[:, 0, 1, :]), op=ALU.subtract)
-                TT(out=dst(6)[:, 0], in0=jy(sd[:, 0, 0, :]), in1=jy(sd[:, 1, 1, :]), op=ALU.subtract)
-                TT(out=dst(6)[:, 1], in0=jy(sd[:, 1, 0, :]), in1=jy(sd[:, 0, 1, :]), op=ALU.add)
-                pp = fft.tile([P, 2, x8], F32, tag="pp")
-                mm = fft.tile([P, 2, x8], F32, tag="mm")
-                TT(out=pp[:], in0=d[:, 0, 1:4:2, :], in1=d[:, 1, 1:4:2, :], op=ALU.add)
-                TT(out=mm[:], in0=d[:, 1, 1:4:2, :], in1=d[:, 0, 1:4:2, :], op=ALU.subtract)
+                tensor_tensor(out=ss[:], in0=s[:, :, 0:2, :], in1=s[:, :, 2:4, :], op=ALU.add)
+                tensor_tensor(out=sd[:], in0=s[:, :, 0:2, :], in1=s[:, :, 2:4, :], op=ALU.subtract)
+                tensor_tensor(out=dst[:, :, :, 0, :], in0=rjy(ss[:, :, 0, :]), in1=rjy(ss[:, :, 1, :]), op=ALU.add)
+                tensor_tensor(out=dst[:, :, :, 4, :], in0=rjy(ss[:, :, 0, :]), in1=rjy(ss[:, :, 1, :]), op=ALU.subtract)
+                tensor_tensor(out=dst[:, 0, :, 2, :], in0=jy(sd[:, 0, 0, :]), in1=jy(sd[:, 1, 1, :]), op=ALU.add)
+                tensor_tensor(out=dst[:, 1, :, 2, :], in0=jy(sd[:, 1, 0, :]), in1=jy(sd[:, 0, 1, :]), op=ALU.subtract)
+                tensor_tensor(out=dst[:, 0, :, 6, :], in0=jy(sd[:, 0, 0, :]), in1=jy(sd[:, 1, 1, :]), op=ALU.subtract)
+                tensor_tensor(out=dst[:, 1, :, 6, :], in0=jy(sd[:, 1, 0, :]), in1=jy(sd[:, 0, 1, :]), op=ALU.add)
+                plus = fft.tile([P, 2, x8], F32, tag="plus")
+                minus = fft.tile([P, 2, x8], F32, tag="minus")
+                tensor_tensor(out=plus[:], in0=d[:, 0, 1:4:2, :], in1=d[:, 1, 1:4:2, :], op=ALU.add)
+                tensor_tensor(out=minus[:], in0=d[:, 1, 1:4:2, :], in1=d[:, 0, 1:4:2, :], op=ALU.subtract)
                 e02p = fft.tile([P, 2, x8], F32, tag="e02p")
                 e02m = fft.tile([P, 2, x8], F32, tag="e02m")
                 e13p = fft.tile([P, 2, x8], F32, tag="e13p")
                 e13m = fft.tile([P, 2, x8], F32, tag="e13m")
-                TT(out=e02p[:, 0, :], in0=d[:, 0, 0, :], in1=d[:, 1, 2, :], op=ALU.add)
-                TT(out=e02p[:, 1, :], in0=d[:, 1, 0, :], in1=d[:, 0, 2, :], op=ALU.subtract)
-                TT(out=e13p[:, 0, :], in0=pp[:, 0, :], in1=mm[:, 1, :], op=ALU.add)
-                TT(out=e13p[:, 1, :], in0=mm[:, 0, :], in1=pp[:, 1, :], op=ALU.subtract)
+                tensor_tensor(out=e02p[:, 0, :], in0=d[:, 0, 0, :], in1=d[:, 1, 2, :], op=ALU.add)
+                tensor_tensor(out=e02p[:, 1, :], in0=d[:, 1, 0, :], in1=d[:, 0, 2, :], op=ALU.subtract)
+                tensor_tensor(out=e13p[:, 0, :], in0=plus[:, 0, :], in1=minus[:, 1, :], op=ALU.add)
+                tensor_tensor(out=e13p[:, 1, :], in0=minus[:, 0, :], in1=plus[:, 1, :], op=ALU.subtract)
                 for r in range(2):
-                    STT(out=dst(1)[:, r], in0=jy(e13p[:, r, :]), scalar=RHO, in1=jy(e02p[:, r, :]), op0=ALU.mult, op1=ALU.add)
-                    STT(out=dst(5)[:, r], in0=jy(e13p[:, r, :]), scalar=-RHO, in1=jy(e02p[:, r, :]), op0=ALU.mult, op1=ALU.add)
-                TT(out=e02m[:, 0, :], in0=d[:, 0, 0, :], in1=d[:, 1, 2, :], op=ALU.subtract)
-                TT(out=e02m[:, 1, :], in0=d[:, 1, 0, :], in1=d[:, 0, 2, :], op=ALU.add)
-                TT(out=e13m[:, 0, :], in0=pp[:, 0, :], in1=mm[:, 1, :], op=ALU.subtract)
-                TT(out=e13m[:, 1, :], in0=mm[:, 0, :], in1=pp[:, 1, :], op=ALU.add)
-                STT(out=dst(3)[:, 0], in0=jy(e13m[:, 1, :]), scalar=RHO, in1=jy(e02m[:, 0, :]), op0=ALU.mult, op1=ALU.add)
-                STT(out=dst(3)[:, 1], in0=jy(e13m[:, 0, :]), scalar=-RHO, in1=jy(e02m[:, 1, :]), op0=ALU.mult, op1=ALU.add)
-                STT(out=dst(7)[:, 0], in0=jy(e13m[:, 1, :]), scalar=-RHO, in1=jy(e02m[:, 0, :]), op0=ALU.mult, op1=ALU.add)
-                STT(out=dst(7)[:, 1], in0=jy(e13m[:, 0, :]), scalar=RHO, in1=jy(e02m[:, 1, :]), op0=ALU.mult, op1=ALU.add)
+                    mul_add(out=dst[:, r, :, 1, :], in0=jy(e13p[:, r, :]), scalar=RHO, in1=jy(e02p[:, r, :]), op0=ALU.mult, op1=ALU.add)
+                    mul_add(out=dst[:, r, :, 5, :], in0=jy(e13p[:, r, :]), scalar=-RHO, in1=jy(e02p[:, r, :]), op0=ALU.mult, op1=ALU.add)
+                tensor_tensor(out=e02m[:, 0, :], in0=d[:, 0, 0, :], in1=d[:, 1, 2, :], op=ALU.subtract)
+                tensor_tensor(out=e02m[:, 1, :], in0=d[:, 1, 0, :], in1=d[:, 0, 2, :], op=ALU.add)
+                tensor_tensor(out=e13m[:, 0, :], in0=plus[:, 0, :], in1=minus[:, 1, :], op=ALU.subtract)
+                tensor_tensor(out=e13m[:, 1, :], in0=minus[:, 0, :], in1=plus[:, 1, :], op=ALU.add)
+                mul_add(out=dst[:, 0, :, 3, :], in0=jy(e13m[:, 1, :]), scalar=RHO, in1=jy(e02m[:, 0, :]), op0=ALU.mult, op1=ALU.add)
+                mul_add(out=dst[:, 1, :, 3, :], in0=jy(e13m[:, 0, :]), scalar=-RHO, in1=jy(e02m[:, 1, :]), op0=ALU.mult, op1=ALU.add)
+                mul_add(out=dst[:, 0, :, 7, :], in0=jy(e13m[:, 1, :]), scalar=-RHO, in1=jy(e02m[:, 0, :]), op0=ALU.mult, op1=ALU.add)
+                mul_add(out=dst[:, 1, :, 7, :], in0=jy(e13m[:, 0, :]), scalar=RHO, in1=jy(e02m[:, 1, :]), op0=ALU.mult, op1=ALU.add)
                 if l > 1:
-                    shape = [P, 2, 7 * l, y]
-                    y7c = y7[:].rearrange("p r (c y) -> p r c y", c=7 * l)
-                    m2 = fft.tile([P, 2, 7 * x8], F32, tag="m2")
-                    TT(out=m2[:].rearrange("p r (c y) -> p r c y", c=7 * l), in0=y7c,
-                       in1=tw.rearrange("p (a b) c -> p a b c", b=2)[:, :, 1, :].unsqueeze(3).to_broadcast(shape), op=ALU.mult)
-                    TT(out=y7c, in0=y7c, in1=tw[:, 0:1, :].unsqueeze(3).to_broadcast(shape), op=ALU.mult)
-                    m1v = y7[:].rearrange("p r (j z) -> p r j z", j=l)
-                    m2v = m2[:].rearrange("p r (j z) -> p r j z", j=l)
-                    nz = nxt[:].rearrange("p r (j z) -> p r j z", j=l)
-                    TT(out=nz[:, 0, :, y:8 * y], in0=m1v[:, 0, :, :], in1=m2v[:, 1, :, :], op=ALU.add)
-                    TT(out=nz[:, 1, :, y:8 * y], in0=m1v[:, 1, :, :], in1=m2v[:, 0, :, :], op=ALU.add)
-                cur = nxt
-            fin = cur[:].rearrange("p r (h y) -> p r h y", h=8)
-            for first, step in GROUPS:
-                nc.scalar.activation(out=fin[:, :, first:8:step, :], in_=fin[:, :, first:8:step, :], func=AF.Square)
+                    shape = [P, l - 1, 7, y]
+                    cross = fft.tile([P, 2, l - 1, 7, y], F32, tag="cross")
+                    for r in range(2):
+                        tensor_tensor(out=cross[:, r, :, :, :], in0=dst[:, r, 1:l, 1:8, :],
+                                      in1=twiddle[:, 1 + 2 * r, 1:l, :].unsqueeze(3).to_broadcast(shape), op=ALU.mult)
+                    for r in range(2):
+                        tensor_tensor(out=dst[:, r, 1:l, 1:8, :], in0=dst[:, r, 1:l, 1:8, :],
+                                      in1=twiddle[:, 0, 1:l, :].unsqueeze(3).to_broadcast(shape), op=ALU.mult)
+                    for r in range(2):
+                        tensor_tensor(out=dst[:, r, 1:l, 1:8, :], in0=dst[:, r, 1:l, 1:8, :], in1=cross[:, 1 - r, :, :, :], op=ALU.add)
+                src = dst_tile
+            spectrum = v[:].rearrange("p r (h y) -> p r h y", h=8)
+            for first, step in EIGHTHS:
+                nc.scalar.activation(out=spectrum[:, :, first:8:step, :], in_=spectrum[:, :, first:8:step, :], func=AF.Square)
 
-        def finish(b):
-            vin, thq, sq0 = per_batch[b]
-            TB = BLK * BATCHES[b][1]
-            sqv = vin[:].rearrange("p r (h k z) -> p r h k z", h=8, k=8)
-            pw = fft.tile([P, G, 4, TB], F32, tag="pw")
-            pwv = pw[:].rearrange("p (h k) s t -> p h k (s t)", h=8)
-            TT(out=pw[:, :, 0, :], in0=sq0[:, 0, :, :], in1=sq0[:, 1, :, :], op=ALU.add)
-            for first, step in GROUPS:
-                TT(out=pwv[:, first:8:step, :, TB:4 * TB], in0=sqv[:, 0, first:8:step, :, :], in1=sqv[:, 1, first:8:step, :, :], op=ALU.add)
-            thv = thq[:].rearrange("p h g t -> p g h t")
+        def compare(b):
+            v, th, sq0 = per_batch[b]
+            tb = BLK * BATCHES[b][1]
+            squares = v[:].rearrange("p r (h k z) -> p r h k z", h=8, k=8)
+            power = fft.tile([P, G, 4, tb], F32, tag="power")
+            power_eighths = power[:].rearrange("p (h k) s t -> p h k (s t)", h=8)
+            tensor_tensor(out=power[:, :, 0, :], in0=sq0[:, 0, :, :], in1=sq0[:, 1, :, :], op=ALU.add)
+            for first, step in EIGHTHS:
+                tensor_tensor(out=power_eighths[:, first:8:step, :, tb:4 * tb], in0=squares[:, 0, first:8:step, :, :],
+                              in1=squares[:, 1, first:8:step, :, :], op=ALU.add)
+            th_view = th[:].rearrange("p h g t -> p g h t")
             for sig in range(2):
-                half = pw[:, :, 2 * sig:2 * sig + 2, :]
-                TT(out=half, in0=half, in1=thv, op=ALU.subtract)
+                of_sig = power[:, :, 2 * sig:2 * sig + 2, :]
+                tensor_tensor(out=of_sig, in0=of_sig, in1=th_view, op=ALU.subtract)
             for sig in range(2):
-                half = pw[:, :, 2 * sig:2 * sig + 2, :]
-                nc.scalar.activation(out=half, in_=half, func=AF.Square, accum_out=acc_d[:, sig, b:b + 1])
+                of_sig = power[:, :, 2 * sig:2 * sig + 2, :]
+                nc.scalar.activation(out=of_sig, in_=of_sig, func=AF.Square, accum_out=d2_sums[:, sig, b:b + 1])
 
-        for i in range(BATCHES[2][0]):
-            front(i)
-        for b in range(NB):
-            stages(b)
-            finish(b)
-            if b + 2 < NB:
-                for i in range(BATCHES[b + 2][0], BATCHES[b + 2][0] + BATCHES[b + 2][1]):
-                    front(i)
+        def blocks_of(b):
+            return range(BATCHES[b][0], BATCHES[b][0] + BATCHES[b][1])
+
+        for b in range(2):
+            for i in blocks_of(b):
+                network(i)
+                inputs(i)
+            for i in blocks_of(b):
+                matrices(i)
+        for b in range(len(BATCHES)):
+            transforms(b)
+            compare(b)
+            if b + 2 < len(BATCHES):
+                for i in blocks_of(b + 2):
+                    network(i)
+                    inputs(i)
+                for i in blocks_of(b + 2):
+                    matrices(i)
+
+        r0 = keep.tile([P, 2, TILES], F32)
+        for sig in range(2):
+            for t in range(TILES):
+                x_squares = stage.tile([P, N], F32)
+                nc.scalar.activation(out=x_squares[:], in_=x_rows[:, sig, t, :], func=AF.Square, accum_out=r0[:, sig, t:t + 1])
 
         sums = keep.tile([P, P], F32)
         nc.vector.memset(sums[:], 0.0)
-        acc_r = keep.tile([P, 2], F32)
-        junk2 = keep.tile([P, TILES], F32)
+        r0_sums = keep.tile([P, 2], F32)
+        r0_squares = keep.tile([P, TILES], F32)
         for sig in range(2):
-            nc.scalar.activation(out=junk2[:], in_=r0[:, sig, :], func=AF.Square, accum_out=acc_r[:, sig:sig + 1])
-        sum_d = keep.tile([P, 2], F32)
-        nc.vector.tensor_reduce(out=sum_d[:], in_=acc_d[:], axis=AX.X, op=ALU.add)
-        nc.vector.scalar_tensor_tensor(out=sums[:, 0:2], in0=sum_d[:], scalar=1.0 / 128.0, in1=acc_r[:], op0=ALU.mult, op1=ALU.subtract)
-        pfin = psum.tile([P, P], F32, tag="ps")
-        nc.tensor.transpose(pfin[:], sums[:], ident[:])
-        tot = keep.tile([P, 1], F32)
-        nc.vector.tensor_reduce(out=tot[:], in_=pfin[:], axis=AX.X, op=ALU.add)
-        res = keep.tile([P, 1], F32)
-        nc.vector.tensor_scalar(out=res[:], in0=tot[:], scalar1=1.0 / (2.0 * B * LAGS), scalar2=None, op0=ALU.mult)
-        nc.sync.dma_start(out=out_1.rearrange("(a b) -> a b", a=1), in_=res[0:1, 0:1])
-        nc.sync.dma_start(out=out_3.rearrange("(a b) -> a b", a=1), in_=res[1:2, 0:1])
+            nc.scalar.activation(out=r0_squares[:], in_=r0[:, sig, :], func=AF.Square, accum_out=r0_sums[:, sig:sig + 1])
+        d2_total = keep.tile([P, 2], F32)
+        nc.vector.tensor_reduce(out=d2_total[:], in_=d2_sums[:], axis=AX.X, op=ALU.add)
+        mul_add(out=sums[:, 0:2], in0=d2_total[:], scalar=1.0 / 128.0, in1=r0_sums[:], op0=ALU.mult, op1=ALU.subtract)
+        sums_t = ps_spec.tile([P, P], F32, tag="spec")
+        nc.tensor.transpose(sums_t[:], sums[:], ident[:])
+        total = keep.tile([P, 1], F32)
+        nc.vector.tensor_reduce(out=total[:], in_=sums_t[:], axis=AX.X, op=ALU.add)
+        err = keep.tile([P, 1], F32)
+        nc.vector.tensor_scalar(out=err[:], in0=total[:], scalar1=1.0 / (2.0 * B * LAGS), scalar2=None, op0=ALU.mult)
+        nc.sync.dma_start(out=out_1.rearrange("(a b) -> a b", a=1), in_=err[0:1, 0:1])
+        nc.sync.dma_start(out=out_3.rearrange("(a b) -> a b", a=1), in_=err[1:2, 0:1])

@@ -25,7 +25,7 @@ NBLK = TILES // BLK
 G = 64
 FAST = ((0, 1), (1, 0), (1, 1))
 BATCHES = ((0, 1), (1, 2), (3, 2), (5, 2), (7, 1))
-SHARED = 2
+SHARED = 3
 EIGHTHS = ((0, 2), (1, 4), (3, 4))
 RHO = math.sqrt(0.5)
 

@@ -28,6 +28,7 @@ BATCHES = ((0, 1), (1, 2), (3, 2), (5, 2), (7, 1))
 SHARED = 3
 EIGHTHS = ((0, 2), (1, 4), (3, 4))
 RHO = math.sqrt(0.5)
+MEAN = 2.0 * B * LAGS
 
 FLOPS = 2 * B * H * (H + N) + 2 * 2 * B * (N * LAGS // 2)
 
@@ -116,7 +117,7 @@ def tile_qdtssolveronnx_pa_kernel(tc, h1, w_hid2, b_hid2, w_out, b_out, norm_roo
                                 op0=ALU.mult, op1=ALU.add)
         nc.vector.tensor_scalar(out=mat_phase[:, G:2 * G], in0=freq[:, 0, :], scalar1=p_float[:, 0:1], scalar2=256.0,
                                 op0=ALU.mult, op1=ALU.add)
-        nc.vector.tensor_scalar(out=mat_phase[:, 2 * G:4 * G], in0=freq[:].rearrange("p h g -> p (h g)"), scalar1=p_float[:, 1:2],
+        nc.vector.tensor_scalar(out=mat_phase[:, 2 * G:4 * G], in0=freq[:].rearrange("p f g -> p (f g)"), scalar1=p_float[:, 1:2],
                                 scalar2=float(COS), op0=ALU.mult, op1=ALU.add)
         mat_table = sines(mat_phase[:], 4 * G + 4, "mat")
         x_matrix = mat_table[:, 0:2 * G]
@@ -271,7 +272,7 @@ def tile_qdtssolveronnx_pa_kernel(tc, h1, w_hid2, b_hid2, w_out, b_out, norm_roo
                     nc.tensor.matmul(out=th_acc[:, t, 0:P - 1], lhsT=t_cols[:, t, :], rhs=t_matrix[:, 0:P - 1], start=True, stop=True)
                 else:
                     nc.tensor.matmul(out=th_acc[:, t, :], lhsT=t_cols[:, t, :], rhs=t_matrix[:], start=True, stop=True)
-            nc.scalar.copy(out=th[:, :, :, sub].rearrange("p h g t -> p (h g) t"), in_=th_acc[:].rearrange("p t c -> p c t"))
+            nc.scalar.copy(out=th[:, :, :, sub].rearrange("p f g t -> p (f g) t"), in_=th_acc[:].rearrange("p t c -> p c t"))
             if i == NBLK - 1:
                 products = stage.tile([P, N], F32)
                 tensor_tensor(out=products[:], in0=t_pad[:, TILES - 1, :], in1=last_col[:], op=ALU.mult)
@@ -292,39 +293,39 @@ def tile_qdtssolveronnx_pa_kernel(tc, h1, w_hid2, b_hid2, w_out, b_out, norm_roo
                     return ap.rearrange("p r (j y) -> p r j y", j=l)
 
                 x = src[:].rearrange("p r (h x) -> p r h x", h=8)
-                s = fft.tile([P, 2, 4, x8], F32, tag="s")
-                d = fft.tile([P, 2, 4, x8], F32, tag="d")
-                tensor_tensor(out=s[:], in0=x[:, :, 0:4, :], in1=x[:, :, 4:8, :], op=ALU.add)
-                tensor_tensor(out=d[:], in0=x[:, :, 0:4, :], in1=x[:, :, 4:8, :], op=ALU.subtract)
+                add4 = fft.tile([P, 2, 4, x8], F32, tag="add4")
+                sub4 = fft.tile([P, 2, 4, x8], F32, tag="sub4")
+                tensor_tensor(out=add4[:], in0=x[:, :, 0:4, :], in1=x[:, :, 4:8, :], op=ALU.add)
+                tensor_tensor(out=sub4[:], in0=x[:, :, 0:4, :], in1=x[:, :, 4:8, :], op=ALU.subtract)
                 dst_tile = fft.tile([P, 2, G * q], F32, tag="mid", name="mid") if l > 1 else v
                 dst = dst_tile[:].rearrange("p r (j h y) -> p r j h y", j=l, h=8)
-                ss = fft.tile([P, 2, 2, x8], F32, tag="ss")
-                sd = fft.tile([P, 2, 2, x8], F32, tag="sd")
-                tensor_tensor(out=ss[:], in0=s[:, :, 0:2, :], in1=s[:, :, 2:4, :], op=ALU.add)
-                tensor_tensor(out=sd[:], in0=s[:, :, 0:2, :], in1=s[:, :, 2:4, :], op=ALU.subtract)
-                tensor_tensor(out=dst[:, :, :, 0, :], in0=rjy(ss[:, :, 0, :]), in1=rjy(ss[:, :, 1, :]), op=ALU.add)
-                tensor_tensor(out=dst[:, :, :, 4, :], in0=rjy(ss[:, :, 0, :]), in1=rjy(ss[:, :, 1, :]), op=ALU.subtract)
-                tensor_tensor(out=dst[:, 0, :, 2, :], in0=jy(sd[:, 0, 0, :]), in1=jy(sd[:, 1, 1, :]), op=ALU.add)
-                tensor_tensor(out=dst[:, 1, :, 2, :], in0=jy(sd[:, 1, 0, :]), in1=jy(sd[:, 0, 1, :]), op=ALU.subtract)
-                tensor_tensor(out=dst[:, 0, :, 6, :], in0=jy(sd[:, 0, 0, :]), in1=jy(sd[:, 1, 1, :]), op=ALU.subtract)
-                tensor_tensor(out=dst[:, 1, :, 6, :], in0=jy(sd[:, 1, 0, :]), in1=jy(sd[:, 0, 1, :]), op=ALU.add)
+                add2 = fft.tile([P, 2, 2, x8], F32, tag="add2")
+                sub2 = fft.tile([P, 2, 2, x8], F32, tag="sub2")
+                tensor_tensor(out=add2[:], in0=add4[:, :, 0:2, :], in1=add4[:, :, 2:4, :], op=ALU.add)
+                tensor_tensor(out=sub2[:], in0=add4[:, :, 0:2, :], in1=add4[:, :, 2:4, :], op=ALU.subtract)
+                tensor_tensor(out=dst[:, :, :, 0, :], in0=rjy(add2[:, :, 0, :]), in1=rjy(add2[:, :, 1, :]), op=ALU.add)
+                tensor_tensor(out=dst[:, :, :, 4, :], in0=rjy(add2[:, :, 0, :]), in1=rjy(add2[:, :, 1, :]), op=ALU.subtract)
+                tensor_tensor(out=dst[:, 0, :, 2, :], in0=jy(sub2[:, 0, 0, :]), in1=jy(sub2[:, 1, 1, :]), op=ALU.add)
+                tensor_tensor(out=dst[:, 1, :, 2, :], in0=jy(sub2[:, 1, 0, :]), in1=jy(sub2[:, 0, 1, :]), op=ALU.subtract)
+                tensor_tensor(out=dst[:, 0, :, 6, :], in0=jy(sub2[:, 0, 0, :]), in1=jy(sub2[:, 1, 1, :]), op=ALU.subtract)
+                tensor_tensor(out=dst[:, 1, :, 6, :], in0=jy(sub2[:, 1, 0, :]), in1=jy(sub2[:, 0, 1, :]), op=ALU.add)
                 plus = fft.tile([P, 2, x8], F32, tag="plus")
                 minus = fft.tile([P, 2, x8], F32, tag="minus")
-                tensor_tensor(out=plus[:], in0=d[:, 0, 1:4:2, :], in1=d[:, 1, 1:4:2, :], op=ALU.add)
-                tensor_tensor(out=minus[:], in0=d[:, 1, 1:4:2, :], in1=d[:, 0, 1:4:2, :], op=ALU.subtract)
+                tensor_tensor(out=plus[:], in0=sub4[:, 0, 1:4:2, :], in1=sub4[:, 1, 1:4:2, :], op=ALU.add)
+                tensor_tensor(out=minus[:], in0=sub4[:, 1, 1:4:2, :], in1=sub4[:, 0, 1:4:2, :], op=ALU.subtract)
                 e02p = fft.tile([P, 2, x8], F32, tag="e02p")
                 e02m = fft.tile([P, 2, x8], F32, tag="e02m")
                 e13p = fft.tile([P, 2, x8], F32, tag="e13p")
                 e13m = fft.tile([P, 2, x8], F32, tag="e13m")
-                tensor_tensor(out=e02p[:, 0, :], in0=d[:, 0, 0, :], in1=d[:, 1, 2, :], op=ALU.add)
-                tensor_tensor(out=e02p[:, 1, :], in0=d[:, 1, 0, :], in1=d[:, 0, 2, :], op=ALU.subtract)
+                tensor_tensor(out=e02p[:, 0, :], in0=sub4[:, 0, 0, :], in1=sub4[:, 1, 2, :], op=ALU.add)
+                tensor_tensor(out=e02p[:, 1, :], in0=sub4[:, 1, 0, :], in1=sub4[:, 0, 2, :], op=ALU.subtract)
                 tensor_tensor(out=e13p[:, 0, :], in0=plus[:, 0, :], in1=minus[:, 1, :], op=ALU.add)
                 tensor_tensor(out=e13p[:, 1, :], in0=minus[:, 0, :], in1=plus[:, 1, :], op=ALU.subtract)
                 for r in range(2):
                     mul_add(out=dst[:, r, :, 1, :], in0=jy(e13p[:, r, :]), scalar=RHO, in1=jy(e02p[:, r, :]), op0=ALU.mult, op1=ALU.add)
                     mul_add(out=dst[:, r, :, 5, :], in0=jy(e13p[:, r, :]), scalar=-RHO, in1=jy(e02p[:, r, :]), op0=ALU.mult, op1=ALU.add)
-                tensor_tensor(out=e02m[:, 0, :], in0=d[:, 0, 0, :], in1=d[:, 1, 2, :], op=ALU.subtract)
-                tensor_tensor(out=e02m[:, 1, :], in0=d[:, 1, 0, :], in1=d[:, 0, 2, :], op=ALU.add)
+                tensor_tensor(out=e02m[:, 0, :], in0=sub4[:, 0, 0, :], in1=sub4[:, 1, 2, :], op=ALU.subtract)
+                tensor_tensor(out=e02m[:, 1, :], in0=sub4[:, 1, 0, :], in1=sub4[:, 0, 2, :], op=ALU.add)
                 tensor_tensor(out=e13m[:, 0, :], in0=plus[:, 0, :], in1=minus[:, 1, :], op=ALU.subtract)
                 tensor_tensor(out=e13m[:, 1, :], in0=minus[:, 0, :], in1=plus[:, 1, :], op=ALU.add)
                 mul_add(out=dst[:, 0, :, 3, :], in0=jy(e13m[:, 1, :]), scalar=RHO, in1=jy(e02m[:, 0, :]), op0=ALU.mult, op1=ALU.add)
@@ -357,13 +358,14 @@ def tile_qdtssolveronnx_pa_kernel(tc, h1, w_hid2, b_hid2, w_out, b_out, norm_roo
             for first, step in EIGHTHS:
                 tensor_tensor(out=power_eighths[:, first:8:step, :, tb:4 * tb], in0=squares[:, 0, first:8:step, :, :],
                               in1=squares[:, 1, first:8:step, :, :], op=ALU.add)
-            th_view = th[:].rearrange("p h g t -> p g h t")
+            th_view = th[:].rearrange("p f g t -> p g f t")
             for sig in range(2):
                 of_sig = power[:, :, 2 * sig:2 * sig + 2, :]
                 tensor_tensor(out=of_sig, in0=of_sig, in1=th_view, op=ALU.subtract)
             for sig in range(2):
                 of_sig = power[:, :, 2 * sig:2 * sig + 2, :]
-                nc.scalar.activation(out=of_sig, in_=of_sig, func=AF.Square, accum_out=d2_sums[:, sig, b:b + 1])
+                nc.scalar.activation(out=of_sig, in_=of_sig, func=AF.Square, scale=1.0 / math.sqrt(128.0 * MEAN),
+                                     accum_out=d2_sums[:, sig, b:b + 1])
 
         def blocks_of(b):
             return range(BATCHES[b][0], BATCHES[b][0] + BATCHES[b][1])
@@ -395,15 +397,14 @@ def tile_qdtssolveronnx_pa_kernel(tc, h1, w_hid2, b_hid2, w_out, b_out, norm_roo
         r0_sums = keep.tile([P, 2], F32)
         r0_squares = keep.tile([P, TILES], F32)
         for sig in range(2):
-            nc.scalar.activation(out=r0_squares[:], in_=r0[:, sig, :], func=AF.Square, accum_out=r0_sums[:, sig:sig + 1])
+            nc.scalar.activation(out=r0_squares[:], in_=r0[:, sig, :], func=AF.Square, scale=1.0 / math.sqrt(MEAN),
+                                 accum_out=r0_sums[:, sig:sig + 1])
         d2_total = keep.tile([P, 2], F32)
         nc.vector.tensor_reduce(out=d2_total[:], in_=d2_sums[:], axis=AX.X, op=ALU.add)
-        mul_add(out=sums[:, 0:2], in0=d2_total[:], scalar=1.0 / 128.0, in1=r0_sums[:], op0=ALU.mult, op1=ALU.subtract)
+        tensor_tensor(out=sums[:, 0:2], in0=d2_total[:], in1=r0_sums[:], op=ALU.subtract)
         sums_t = ps_spec.tile([P, P], F32, tag="spec")
         nc.tensor.transpose(sums_t[:], sums[:], ident[:])
-        total = keep.tile([P, 1], F32)
-        nc.vector.tensor_reduce(out=total[:], in_=sums_t[:], axis=AX.X, op=ALU.add)
         err = keep.tile([P, 1], F32)
-        nc.vector.tensor_scalar(out=err[:], in0=total[:], scalar1=1.0 / (2.0 * B * LAGS), scalar2=None, op0=ALU.mult)
+        nc.vector.tensor_reduce(out=err[:], in_=sums_t[:], axis=AX.X, op=ALU.add)
         nc.sync.dma_start(out=out_1.rearrange("(a b) -> a b", a=1), in_=err[0:1, 0:1])
         nc.sync.dma_start(out=out_3.rearrange("(a b) -> a b", a=1), in_=err[1:2, 0:1])

import math
from contextlib import ExitStack

import concourse.mybir as mybir
from concourse.masks import make_identity

F32 = mybir.dt.float32
BF16 = mybir.dt.bfloat16
I32 = mybir.dt.int32
U32 = mybir.dt.uint32
U8 = mybir.dt.uint8
FP8X4 = mybir.dt.float8_e4m3fn_x4
ALU = mybir.AluOpType
AF = mybir.ActivationFunctionType
AX = mybir.AxisListType

P = 128
B = 4096
H = 512
N = 128
LAGS = 127
TILES = B // P
BLK = 4
NBLK = TILES // BLK
G = 64
FAST = ((0, 1), (1, 0), (1, 1))
BATCHES = ((0, 1), (1, 2), (3, 2), (5, 2), (7, 1))
SHARED = 3
EIGHTHS = ((0, 2), (1, 4), (3, 4))
RHO = math.sqrt(0.5)
MEAN = 2.0 * B * LAGS

FLOPS = 2 * B * H * (H + N) + 2 * 2 * B * (N * LAGS // 2)


def tile_qdtssolveronnx_pa_kernel(tc, h1, w_hid2, b_hid2, w_out, b_out, norm_root, T, out_0, out_1, out_2, out_3):
    nc = tc.nc
    tensor_tensor = nc.vector.tensor_tensor
    mul_add = nc.vector.scalar_tensor_tensor
    with ExitStack() as ctx:
        keep = ctx.enter_context(tc.tile_pool(name="keep", bufs=1))
        h1_pool = ctx.enter_context(tc.tile_pool(name="h1_pool", bufs=3))
        stage = ctx.enter_context(tc.tile_pool(name="stage", bufs=2))
        z_pool = ctx.enter_context(tc.tile_pool(name="z_pool", bufs=3))
        batch_pool = ctx.enter_context(tc.tile_pool(name="batch_pool", bufs=2))
        fft = ctx.enter_context(tc.tile_pool(name="fft", bufs=1))
        ps_in = ctx.enter_context(tc.psum_pool(name="ps_in", bufs=1))
        ps_h2 = ctx.enter_context(tc.psum_pool(name="ps_h2", bufs=2))
        ps_x = ctx.enter_context(tc.psum_pool(name="ps_x", bufs=1))
        ps_spec = ctx.enter_context(tc.psum_pool(name="ps_spec", bufs=4))

        w1_sb = keep.tile([P, 4, H], BF16)
        nc.sync.dma_start(out=w1_sb[:], in_=w_hid2.rearrange("(p c) k -> p c k", c=4))
        h1_rows = h1.rearrange("(p t) k -> p t k", t=TILES)
        h1_tiles = {}

        def load_h1(i):
            h1_sb = h1_pool.tile([P, BLK, H], BF16, name="h1_sb")
            nc.sync.dma_start(out=h1_sb[:], in_=h1_rows[:, BLK * i:BLK * (i + 1), :])
            h1_tiles[i] = h1_sb

        b1_bf = keep.tile([P, 4], BF16)
        b2_bf = keep.tile([P, 1], BF16)
        nr_bf = keep.tile([P, TILES], BF16)
        with nc.allow_non_contiguous_dma(reason="three short vectors, a few bytes a partition"):
            nc.scalar.dma_start(out=b1_bf[:], in_=b_hid2.rearrange("(p c) -> p c", c=4))
            nc.scalar.dma_start(out=b2_bf[:], in_=b_out.rearrange("(p o) -> p o", o=1))
            nc.scalar.dma_start(out=nr_bf[:], in_=norm_root.rearrange("(p t) o -> p (t o)", t=TILES))
        t_pad = keep.tile([P, TILES, N], BF16)
        nc.vector.memset(t_pad[:], 0.0)
        ident = keep.tile([P, P], F32)
        make_identity(nc, ident[:])
        ident_bf = keep.tile([P, P], BF16)
        make_identity(nc, ident_bf[:])
        load_h1(0)
        w2_sb = keep.tile([P, H], BF16)
        nc.sync.dma_start(out=w2_sb[:], in_=w_out)
        load_h1(1)
        nc.sync.dma_start(out=t_pad[:, :, 0:LAGS], in_=T.rearrange("(p t) c -> p t c", t=TILES))

        def sines(phase, width, name):
            nc.vector.tensor_single_scalar(out=phase, in_=phase, scalar=511, op=ALU.bitwise_and)
            angle = fft.tile([P, width], F32, name=name + "_angle", tag="mid")
            nc.vector.tensor_scalar(out=angle[:], in0=phase, scalar1=-256.0, scalar2=None, op0=ALU.add)
            edge = fft.tile([P, width], F32, name=name + "_edge", tag="cross")
            nc.vector.tensor_scalar(out=edge[:], in0=angle[:], scalar1=-256.0, scalar2=256.0, op0=ALU.is_equal, op1=ALU.mult)
            nc.vector.tensor_tensor(out=angle[:], in0=angle[:], in1=edge[:], op=ALU.add)
            table = keep.tile([P, width], F32, name=name + "_table")
            nc.scalar.activation(out=table[:], in_=angle[:], func=AF.Sin, scale=math.pi / 256.0)
            return table

        COS = 256 + 128

        W_TW = 4 * 56
        row_phase = keep.tile([P, W_TW + N], I32)
        tw_phase = row_phase[:, 0:W_TW].rearrange("p (k j h) -> p k j h", k=4, h=7)
        for h in range(1, 8):
            nc.gpsimd.iota(tw_phase[:, :, :, h - 1], pattern=[[128, 4], [8 * h, 8]], base=COS, channel_multiplier=0)
        LAST_FREQ = 4 * (N - 1) + 1
        nc.gpsimd.iota(row_phase[:, W_TW:W_TW + N], pattern=[[-LAST_FREQ, N]], base=LAGS * LAST_FREQ + COS, channel_multiplier=0)
        row_table = sines(row_phase[:], W_TW + N, "row")
        twiddle = row_table[:, 0:W_TW].rearrange("p (k j h) -> p k j h", k=4, h=7)
        last_col = keep.tile([P, N], F32)
        nc.vector.tensor_scalar(out=last_col[:], in0=row_table[:, W_TW:W_TW + N], scalar1=2.0, scalar2=None, op0=ALU.mult)

        p_index = keep.tile([P, 2], I32)
        nc.gpsimd.iota(p_index[:, 0:1], pattern=[[0, 1]], base=0, channel_multiplier=1)
        nc.gpsimd.iota(p_index[:, 1:2], pattern=[[0, 1]], base=LAGS, channel_multiplier=-1)
        p_float = keep.tile([P, 2], F32)
        nc.vector.tensor_copy(out=p_float[:], in_=p_index[:])
        freq = keep.tile([P, 2, G], I32)
        nc.gpsimd.iota(freq[:], pattern=[[4, 2], [8, G]], base=1, channel_multiplier=0)
        mat_phase = keep.tile([P, 4 * G + 4], I32)
        for hf in range(2):
            nc.gpsimd.iota(mat_phase[:, 4 * G + 2 * hf:4 * G + 2 * hf + 2], pattern=[[128, 2]], base=COS, channel_multiplier=1 + 4 * hf)
        nc.vector.tensor_scalar(out=mat_phase[:, 0:G], in0=freq[:, 0, :], scalar1=p_float[:, 0:1], scalar2=float(COS),
                                op0=ALU.mult, op1=ALU.add)
        nc.vector.tensor_scalar(out=mat_phase[:, G:2 * G], in0=freq[:, 0, :], scalar1=p_float[:, 0:1], scalar2=256.0,
                                op0=ALU.mult, op1=ALU.add)
        nc.vector.tensor_scalar(out=mat_phase[:, 2 * G:4 * G], in0=freq[:].rearrange("p f g -> p (f g)"), scalar1=p_float[:, 1:2],
                                scalar2=float(COS), op0=ALU.mult, op1=ALU.add)
        mat_table = sines(mat_phase[:], 4 * G + 4, "mat")
        x_matrix = mat_table[:, 0:2 * G]
        t_matrix = keep.tile([P, 2 * G], F32)
        nc.vector.tensor_scalar(out=t_matrix[:], in0=mat_table[:, 2 * G:4 * G], scalar1=2.0, scalar2=None, op0=ALU.mult)
        twist = mat_table[:, 4 * G:4 * G + 4]

        b1 = keep.tile([P, 4], F32)
        nc.vector.tensor_copy(out=b1[:], in_=b1_bf[:])
        b2 = keep.tile([P, 1], F32)
        nc.vector.tensor_copy(out=b2[:], in_=b2_bf[:])
        nr = keep.tile([P, TILES], F32)
        nc.vector.tensor_copy(out=nr[:], in_=nr_bf[:])

        w1_grouped = keep.tile([P, 4 * P, 4], BF16, align_bytes=64)
        w1_grouped32 = w1_grouped[:].bitcast(F32)
        w1_words = w1_sb[:].bitcast(F32)
        for a in range(2):
            w1_t = ps_in.tile([P, 2, 2, P], F32, tag="in")
            for u in range(2):
                for c in range(2):
                    nc.tensor.transpose(w1_t[:, u, c, :], w1_words[:, 2 * a + c, P * u:P * (u + 1)], ident[:])
            nc.vector.tensor_copy(out=w1_grouped32[:, 2 * P * a:2 * P * (a + 1), :], in_=w1_t[:].rearrange("q u c m -> q (c m) u"))
        w1_codes = keep.tile([P, 4 * P], U32, align_bytes=64)
        w1_scales = keep.tile([P, 4 * P], U8, align_bytes=64)
        nc.vector.quantize_mx(out=w1_codes[:].bitcast(FP8X4), scales=w1_scales[:], in_=w1_grouped[:].rearrange("q n f -> q (n f)"))
        w2_grouped = keep.tile([P, P, 4], BF16, align_bytes=64)
        w2_words = w2_sb[:].bitcast(F32).rearrange("p (m u) -> p u m", u=2)
        w2_t = ps_in.tile([P, 2, P], F32, tag="in")
        for u in range(2):
            nc.tensor.transpose(w2_t[:, u, :], w2_words[:, u, :], ident[:])
        nc.vector.tensor_copy(out=w2_grouped[:].bitcast(F32), in_=w2_t[:].rearrange("q u n -> q n u"))
        w2_codes = keep.tile([P, P], U32, align_bytes=64)
        w2_scales = keep.tile([P, P], U8, align_bytes=64)
        nc.vector.quantize_mx(out=w2_codes[:].bitcast(FP8X4), scales=w2_scales[:], in_=w2_grouped[:].rearrange("q n f -> q (n f)"))

        x_rows = keep.tile([P, 2, TILES, N], F32)
        x_out = (out_0.rearrange("(p t) j -> p t j", t=TILES), out_2.rearrange("(p t) j -> p t j", t=TILES))
        d2_sums = keep.tile([P, 2, len(BATCHES)], F32)
        per_batch = {}
        x_cols = {}

        def place(i):
            b = [k for k, (first, count) in enumerate(BATCHES) if first <= i < first + count][0]
            at = BLK * (i - BATCHES[b][0])
            return b, BLK * BATCHES[b][1], slice(at, at + BLK)

        def network(i):
            shared = i < SHARED
            if i + 2 < NBLK:
                load_h1(i + 2)
            h1_words = h1_tiles[i][:].bitcast(F32)
            h1_grouped = stage.tile([P, BLK * P, 4], BF16, align_bytes=64)
            h1_grouped32 = h1_grouped[:].bitcast(F32)
            for a in range(2):
                h1_t = ps_in.tile([P, 2, 2, P], F32, tag="in")
                for u in range(2):
                    for t in range(2):
                        nc.tensor.transpose(h1_t[:, u, t, :], h1_words[:, 2 * a + t, P * u:P * (u + 1)], ident[:])
                if shared:
                    nc.vector.tensor_copy(out=h1_grouped32[:, 2 * P * a:2 * P * (a + 1), :], in_=h1_t[:].rearrange("q u t p -> q (t p) u"))
                else:
                    nc.scalar.copy(out=h1_grouped32[:, 2 * P * a:2 * P * (a + 1), :], in_=h1_t[:].rearrange("q u t p -> q (t p) u"))
            h1_codes = stage.tile([P, BLK * P], U32, align_bytes=64)
            h1_scales = stage.tile([P, BLK * P], U8, align_bytes=64)
            nc.vector.quantize_mx(out=h1_codes[:].bitcast(FP8X4), scales=h1_scales[:], in_=h1_grouped[:].rearrange("q n f -> q (n f)"))

            h2_planes = stage.tile([P, 4, BLK * P], BF16)
            for c in range(4):
                h2_acc = ps_h2.tile([P, BLK * P], F32, tag="h2")
                nc.tensor.matmul_mx(out=h2_acc[:], lhsT=w1_codes[:, P * c:P * (c + 1)].bitcast(FP8X4),
                                    lhsT_scale=w1_scales[:, P * c:P * (c + 1)],
                                    rhs=h1_codes[:].bitcast(FP8X4), rhs_scale=h1_scales[:], start=True, stop=True)
                if shared and c % 2 == 1:
                    nc.vector.tensor_scalar(out=h2_planes[:, c, :], in0=h2_acc[:], scalar1=b1[:, c:c + 1], scalar2=0.0,
                                            op0=ALU.add, op1=ALU.max)
                else:
                    nc.scalar.activation(out=h2_planes[:, c, :], in_=h2_acc[:], func=AF.Relu, bias=b1[:, c:c + 1], scale=1.0)
            h2_grouped = stage.tile([P, BLK * P, 4], BF16, align_bytes=64)
            grouped_runs = h2_grouped[:].rearrange("m (a i) c -> m a c i", i=4)
            plane_runs = h2_planes[:].rearrange("m c (a i) -> m a c i", i=4)
            if shared:
                nc.vector.tensor_copy(out=grouped_runs, in_=plane_runs)
            else:
                nc.scalar.copy(out=grouped_runs, in_=plane_runs)
            h2_codes = stage.tile([P, BLK * P], U32, align_bytes=64)
            h2_scales = stage.tile([P, BLK * P], U8, align_bytes=64)
            nc.vector.quantize_mx(out=h2_codes[:].bitcast(FP8X4), scales=h2_scales[:], in_=h2_grouped[:].rearrange("m n f -> m (n f)"))

            y_acc = ps_x.tile([P, BLK * P], F32, tag="x")
            nc.tensor.matmul_mx(out=y_acc[:], lhsT=w2_codes[:].bitcast(FP8X4), lhsT_scale=w2_scales[:],
                                rhs=h2_codes[:].bitcast(FP8X4), rhs_scale=h2_scales[:], start=True, stop=True)
            y_cols = stage.tile([P, BLK * P], F32)
            nc.scalar.activation(out=y_cols[:], in_=y_acc[:], func=AF.Identity, bias=b2[:, 0:1], scale=1.0)
            y_rows = ps_x.tile([P, BLK, P], F32, tag="x")
            for t in range(BLK):
                nc.tensor.transpose(y_rows[:, t, :], y_cols[:, P * t:P * (t + 1)], ident[:])
            tiles = slice(BLK * i, BLK * (i + 1))
            for t in range(BLK):
                nc.scalar.activation(out=x_rows[:, 0, BLK * i + t, :], in_=y_rows[:, t, :], func=AF.Copy,
                                     scale=nr[:, BLK * i + t:BLK * i + t + 1])
            nc.vector.tensor_scalar(out=x_rows[:, 1, tiles, :], in0=x_rows[:, 0, tiles, :], scalar1=-2.0, scalar2=2.0,
                                    op0=ALU.max, op1=ALU.min)
            for sig in range(2):
                nc.sync.dma_start(out=x_out[sig][:, tiles, :], in_=x_rows[:, sig, tiles, :])

        def inputs(i):
            b, tb, sub = place(i)
            if b not in per_batch:
                v_new = batch_pool.tile([P, 2, G * 3 * tb], F32, name="v")
                th_new = batch_pool.tile([P, 2, G, tb], F32, name="th")
                sq0_new = batch_pool.tile([P, 2, G, tb], F32, name="sq0")
                per_batch[b] = (v_new, th_new, sq0_new)
            v_view = per_batch[b][0][:].rearrange("p r (n s t) -> p r n s t", s=3, t=tb)
            cols = []
            for sig in range(2):
                sig_cols = ps_spec.tile([P, BLK, P], F32, tag="spec", name="sig_cols")
                for t in range(BLK):
                    nc.tensor.transpose(sig_cols[:, t, :], x_rows[:, sig, BLK * i + t, :], ident[:])
                cols.append(sig_cols)
            for s, (sig, hf) in enumerate(FAST):
                for r in range(2):
                    z_cols = z_pool.tile([P, BLK, P], F32, name="z_cols")
                    nc.scalar.activation(out=z_cols[:], in_=cols[sig][:], func=AF.Copy, scale=twist[:, 2 * hf + r:2 * hf + r + 1])
                    z_rows = ps_spec.tile([P, BLK, P], F32, tag="spec", name="z_rows")
                    for t in range(BLK):
                        nc.tensor.transpose(z_rows[:, t, :], z_cols[:, t, :], ident[:])
                    z_high = z_pool.tile([P, G, BLK], F32, name="z_high")
                    nc.scalar.copy(out=z_high[:], in_=z_rows[:, :, G:N].rearrange("p t n -> p n t"))
                    tensor_tensor(out=v_view[:, r, :, s, sub], in0=z_rows[:, :, 0:G].rearrange("p t n -> p n t"), in1=z_high[:], op=ALU.add)
                if s == 0:
                    x_cols[i] = stage.tile([P, BLK, P], F32, name="x_cols")
                    nc.scalar.copy(out=x_cols[i][:], in_=cols[0][:])

        def matrices(i):
            b, tb, sub = place(i)
            v, th, sq0 = per_batch[b]
            spec0 = ps_spec.tile([P, BLK, P], F32, tag="spec")
            for t in range(BLK):
                nc.tensor.matmul(out=spec0[:, t, :], lhsT=x_cols[i][:, t, :], rhs=x_matrix, start=True, stop=True)
            nc.scalar.activation(out=sq0[:, :, :, sub].rearrange("p r g t -> p (r g) t"), in_=spec0[:].rearrange("p t c -> p c t"),
                                 func=AF.Square)
            t_t = ps_spec.tile([P, BLK, P], BF16, tag="spec")
            for t in range(BLK):
                nc.tensor.transpose(t_t[:, t, :], t_pad[:, BLK * i + t, :], ident_bf[:])
            t_cols = stage.tile([P, BLK, P], F32)
            nc.scalar.copy(out=t_cols[:], in_=t_t[:])
            th_acc = ps_spec.tile([P, BLK, P], F32, tag="spec")
            for t in range(BLK):
                if BLK * i + t == TILES - 1:
                    nc.tensor.transpose(th_acc[:, t, :], t_cols[:, t, :], ident[:])
                    nc.tensor.matmul(out=th_acc[:, t, 0:P - 1], lhsT=t_cols[:, t, :], rhs=t_matrix[:, 0:P - 1], start=True, stop=True)
                else:
                    nc.tensor.matmul(out=th_acc[:, t, :], lhsT=t_cols[:, t, :], rhs=t_matrix[:], start=True, stop=True)
            nc.scalar.copy(out=th[:, :, :, sub].rearrange("p f g t -> p (f g) t"), in_=th_acc[:].rearrange("p t c -> p c t"))
            if i == NBLK - 1:
                products = stage.tile([P, N], F32)
                tensor_tensor(out=products[:], in0=t_pad[:, TILES - 1, :], in1=last_col[:], op=ALU.mult)
                nc.vector.tensor_reduce(out=th[:, 1, G - 1, tb - 1:tb], in_=products[:], axis=AX.X, op=ALU.add)

        def transforms(b):
            q = 3 * BLK * BATCHES[b][1]
            x8 = 8 * q
            v = per_batch[b][0]
            src = v
            for l, m in ((8, 1), (1, 8)):
                y = m * q

                def jy(ap):
                    return ap.rearrange("p (j y) -> p j y", j=l)

                def rjy(ap):
                    return ap.rearrange("p r (j y) -> p r j y", j=l)

                x = src[:].rearrange("p r (h x) -> p r h x", h=8)
                add4 = fft.tile([P, 2, 4, x8], F32, tag="add4")
                sub4 = fft.tile([P, 2, 4, x8], F32, tag="sub4")
                tensor_tensor(out=add4[:], in0=x[:, :, 0:4, :], in1=x[:, :, 4:8, :], op=ALU.add)
                tensor_tensor(out=sub4[:], in0=x[:, :, 0:4, :], in1=x[:, :, 4:8, :], op=ALU.subtract)
                dst_tile = fft.tile([P, 2, G * q], F32, tag="mid", name="mid") if l > 1 else v
                dst = dst_tile[:].rearrange("p r (j h y) -> p r j h y", j=l, h=8)
                add2 = fft.tile([P, 2, 2, x8], F32, tag="add2")
                sub2 = fft.tile([P, 2, 2, x8], F32, tag="sub2")
                tensor_tensor(out=add2[:], in0=add4[:, :, 0:2, :], in1=add4[:, :, 2:4, :], op=ALU.add)
                tensor_tensor(out=sub2[:], in0=add4[:, :, 0:2, :], in1=add4[:, :, 2:4, :], op=ALU.subtract)
                tensor_tensor(out=dst[:, :, :, 0, :], in0=rjy(add2[:, :, 0, :]), in1=rjy(add2[:, :, 1, :]), op=ALU.add)
                tensor_tensor(out=dst[:, :, :, 4, :], in0=rjy(add2[:, :, 0, :]), in1=rjy(add2[:, :, 1, :]), op=ALU.subtract)
                tensor_tensor(out=dst[:, 0, :, 2, :], in0=jy(sub2[:, 0, 0, :]), in1=jy(sub2[:, 1, 1, :]), op=ALU.add)
                tensor_tensor(out=dst[:, 1, :, 2, :], in0=jy(sub2[:, 1, 0, :]), in1=jy(sub2[:, 0, 1, :]), op=ALU.subtract)
                tensor_tensor(out=dst[:, 0, :, 6, :], in0=jy(sub2[:, 0, 0, :]), in1=jy(sub2[:, 1, 1, :]), op=ALU.subtract)
                tensor_tensor(out=dst[:, 1, :, 6, :], in0=jy(sub2[:, 1, 0, :]), in1=jy(sub2[:, 0, 1, :]), op=ALU.add)
                plus = fft.tile([P, 2, x8], F32, tag="plus")
                minus = fft.tile([P, 2, x8], F32, tag="minus")
                tensor_tensor(out=plus[:], in0=sub4[:, 0, 1:4:2, :], in1=sub4[:, 1, 1:4:2, :], op=ALU.add)
                tensor_tensor(out=minus[:], in0=sub4[:, 1, 1:4:2, :], in1=sub4[:, 0, 1:4:2, :], op=ALU.subtract)
                e02p = fft.tile([P, 2, x8], F32, tag="e02p")
                e02m = fft.tile([P, 2, x8], F32, tag="e02m")
                e13p = fft.tile([P, 2, x8], F32, tag="e13p")
                e13m = fft.tile([P, 2, x8], F32, tag="e13m")
                tensor_tensor(out=e02p[:, 0, :], in0=sub4[:, 0, 0, :], in1=sub4[:, 1, 2, :], op=ALU.add)
                tensor_tensor(out=e02p[:, 1, :], in0=sub4[:, 1, 0, :], in1=sub4[:, 0, 2, :], op=ALU.subtract)
                tensor_tensor(out=e13p[:, 0, :], in0=plus[:, 0, :], in1=minus[:, 1, :], op=ALU.add)
                tensor_tensor(out=e13p[:, 1, :], in0=minus[:, 0, :], in1=plus[:, 1, :], op=ALU.subtract)
                for r in range(2):
                    mul_add(out=dst[:, r, :, 1, :], in0=jy(e13p[:, r, :]), scalar=RHO, in1=jy(e02p[:, r, :]), op0=ALU.mult, op1=ALU.add)
                    mul_add(out=dst[:, r, :, 5, :], in0=jy(e13p[:, r, :]), scalar=-RHO, in1=jy(e02p[:, r, :]), op0=ALU.mult, op1=ALU.add)
                tensor_tensor(out=e02m[:, 0, :], in0=sub4[:, 0, 0, :], in1=sub4[:, 1, 2, :], op=ALU.subtract)
                tensor_tensor(out=e02m[:, 1, :], in0=sub4[:, 1, 0, :], in1=sub4[:, 0, 2, :], op=ALU.add)
                tensor_tensor(out=e13m[:, 0, :], in0=plus[:, 0, :], in1=minus[:, 1, :], op=ALU.subtract)
                tensor_tensor(out=e13m[:, 1, :], in0=minus[:, 0, :], in1=plus[:, 1, :], op=ALU.add)
                mul_add(out=dst[:, 0, :, 3, :], in0=jy(e13m[:, 1, :]), scalar=RHO, in1=jy(e02m[:, 0, :]), op0=ALU.mult, op1=ALU.add)
                mul_add(out=dst[:, 1, :, 3, :], in0=jy(e13m[:, 0, :]), scalar=-RHO, in1=jy(e02m[:, 1, :]), op0=ALU.mult, op1=ALU.add)
                mul_add(out=dst[:, 0, :, 7, :], in0=jy(e13m[:, 1, :]), scalar=-RHO, in1=jy(e02m[:, 0, :]), op0=ALU.mult, op1=ALU.add)
                mul_add(out=dst[:, 1, :, 7, :], in0=jy(e13m[:, 0, :]), scalar=RHO, in1=jy(e02m[:, 1, :]), op0=ALU.mult, op1=ALU.add)
                if l > 1:
                    shape = [P, l - 1, 7, y]
                    cross = fft.tile([P, 2, l - 1, 7, y], F32, tag="cross")
                    for r in range(2):
                        tensor_tensor(out=cross[:, r, :, :, :], in0=dst[:, r, 1:l, 1:8, :],
                                      in1=twiddle[:, 1 + 2 * r, 1:l, :].unsqueeze(3).to_broadcast(shape), op=ALU.mult)
                    for r in range(2):
                        tensor_tensor(out=dst[:, r, 1:l, 1:8, :], in0=dst[:, r, 1:l, 1:8, :],
                                      in1=twiddle[:, 0, 1:l, :].unsqueeze(3).to_broadcast(shape), op=ALU.mult)
                    for r in range(2):
                        tensor_tensor(out=dst[:, r, 1:l, 1:8, :], in0=dst[:, r, 1:l, 1:8, :], in1=cross[:, 1 - r, :, :, :], op=ALU.add)
                src = dst_tile
            spectrum = v[:].rearrange("p r (h y) -> p r h y", h=8)
            for first, step in EIGHTHS:
                nc.scalar.activation(out=spectrum[:, :, first:8:step, :], in_=spectrum[:, :, first:8:step, :], func=AF.Square)

        def compare(b):
            v, th, sq0 = per_batch[b]
            tb = BLK * BATCHES[b][1]
            squares = v[:].rearrange("p r (h k z) -> p r h k z", h=8, k=8)
            power = fft.tile([P, G, 4, tb], F32, tag="power")
            power_eighths = power[:].rearrange("p (h k) s t -> p h k (s t)", h=8)
            tensor_tensor(out=power[:, :, 0, :], in0=sq0[:, 0, :, :], in1=sq0[:, 1, :, :], op=ALU.add)
            for first, step in EIGHTHS:
                tensor_tensor(out=power_eighths[:, first:8:step, :, tb:4 * tb], in0=squares[:, 0, first:8:step, :, :],
                              in1=squares[:, 1, first:8:step, :, :], op=ALU.add)
            th_view = th[:].rearrange("p f g t -> p g f t")
            for sig in range(2):
                of_sig = power[:, :, 2 * sig:2 * sig + 2, :]
                tensor_tensor(out=of_sig, in0=of_sig, in1=th_view, op=ALU.subtract)
            for sig in range(2):
                of_sig = power[:, :, 2 * sig:2 * sig + 2, :]
                nc.scalar.activation(out=of_sig, in_=of_sig, func=AF.Square, scale=1.0 / math.sqrt(128.0 * MEAN),
                                     accum_out=d2_sums[:, sig, b:b + 1])

        def blocks_of(b):
            return range(BATCHES[b][0], BATCHES[b][0] + BATCHES[b][1])

        for b in range(2):
            for i in blocks_of(b):
                network(i)
                inputs(i)
            for i in blocks_of(b):
                matrices(i)
        for b in range(len(BATCHES)):
            transforms(b)
            compare(b)
            if b + 2 < len(BATCHES):
                for i in blocks_of(b + 2):
                    network(i)
                    inputs(i)
                for i in blocks_of(b + 2):
                    matrices(i)

        r0 = keep.tile([P, 2, TILES], F32)
        for sig in range(2):
            for t in range(TILES):
                x_squares = stage.tile([P, N], F32)
                nc.scalar.activation(out=x_squares[:], in_=x_rows[:, sig, t, :], func=AF.Square, accum_out=r0[:, sig, t:t + 1])

        sums = keep.tile([P, P], F32)
        nc.vector.memset(sums[:], 0.0)
        r0_sums = keep.tile([P, 2], F32)
        r0_squares = keep.tile([P, TILES], F32)
        for sig in range(2):
            nc.scalar.activation(out=r0_squares[:], in_=r0[:, sig, :], func=AF.Square, scale=1.0 / math.sqrt(MEAN),
                                 accum_out=r0_sums[:, sig:sig + 1])
        d2_total = keep.tile([P, 2], F32)
        nc.vector.tensor_reduce(out=d2_total[:], in_=d2_sums[:], axis=AX.X, op=ALU.add)
        tensor_tensor(out=sums[:, 0:2], in0=d2_total[:], in1=r0_sums[:], op=ALU.subtract)
        sums_t = ps_spec.tile([P, P], F32, tag="spec")
        nc.tensor.transpose(sums_t[:], sums[:], ident[:])
        err = keep.tile([P, 1], F32)
        nc.vector.tensor_reduce(out=err[:], in_=sums_t[:], axis=AX.X, op=ALU.add)
        nc.sync.dma_start(out=out_1.rearrange("(a b) -> a b", a=1), in_=err[0:1, 0:1])
        nc.sync.dma_start(out=out_3.rearrange("(a b) -> a b", a=1), in_=err[1:2, 0:1])
